import numpy as np
import ml_dtypes


def mxq(x, axis, fmt="e4m3"):
    dtype, down = {"e4m3": (ml_dtypes.float8_e4m3fn, 7), "e5m2": (ml_dtypes.float8_e5m2, 14)}[fmt]
    v = np.moveaxis(np.asarray(x, np.float32).astype(ml_dtypes.bfloat16).astype(np.float64), axis, -1)
    blocks = v.reshape(v.shape[:-1] + (-1, 32))
    amax = np.abs(blocks).max(-1, keepdims=True)
    byte = np.maximum(np.where(amax > 0, np.frexp(amax)[1] - 1 + 127, 0) - down, 1)
    scale = np.exp2(byte - 127.0)
    codes = (blocks / scale).astype(np.float32).astype(dtype).astype(np.float64)
    return np.moveaxis((codes * scale).reshape(v.shape), -1, axis)


WIDE = False


def mx_kscale(k):
    if not WIDE:
        return np.ones(k)
    levels = np.array([30, -30])
    if k % 512:
        return np.exp2(np.random.permutation(np.resize(levels, k // 32))).repeat(32)
    a = np.empty((k // 512, 16))
    for p in range(k // 512):
        a[p, :8] = np.random.permutation(np.resize(levels, 8))
        for g in range(8):
            far = levels[np.abs(levels - a[p, g]) >= 10]
            a[p, g + 8] = far[np.random.randint(len(far))]
    return np.exp2(a.ravel()).repeat(32)


BF16 = ml_dtypes.bfloat16


def bf(x):
    return np.asarray(x, np.float32).astype(BF16)


def f64(x):
    return np.asarray(x).astype(np.float64)


E2M1 = np.array([0.0, 0.5, 1.0, 1.5, 2.0, 3.0, 4.0, 6.0, -0.0, -0.5, -1.0, -1.5, -2.0, -3.0, -4.0, -6.0])


def pack_weight(w, fmt):
    k, n = w.shape
    w = f64(bf(w)).reshape(k // 32, 32, n)
    amax = np.abs(w).max(1)
    if fmt == "e4m3":
        byte = np.frexp(amax)[1] - 1 + 127 - 7
    else:
        mant, ex = np.frexp(amax / 6.0)
        byte = np.where(mant > 0.5, ex, ex - 1) + 127
    byte = np.clip(np.where(amax > 0, byte, 1), 1, 254)
    scaled = (w * np.exp2(127.0 - byte)[:, None, :]).reshape(k, n).astype(np.float32)
    by_word = np.ascontiguousarray(scaled.reshape(k // 512, 128, 4, n).transpose(0, 1, 3, 2))
    if fmt == "e4m3":
        words = by_word.astype(ml_dtypes.float8_e4m3fn).view(np.uint8)
    else:
        c = by_word.astype(ml_dtypes.float4_e2m1fn).view(np.uint8) & 0xF
        words = c[..., 0::2] | (c[..., 1::2] << 4)
    return np.ascontiguousarray(words), np.ascontiguousarray(byte.astype(np.uint8).reshape(k // 512, 16, n))


def unpack_weight(words, scales, fmt):
    g, p, n, _ = words.shape
    if fmt == "e4m3":
        vals = np.ascontiguousarray(words).view(ml_dtypes.float8_e4m3fn).astype(np.float64)
    else:
        nib = np.empty((g, p, n, 4), np.uint8)
        nib[..., 0::2] = words & 0xF
        nib[..., 1::2] = words >> 4
        vals = E2M1[nib]
    vals = vals * np.repeat(np.exp2(scales.astype(np.float64) - 127.0), 8, axis=1)[..., None]
    return vals.transpose(0, 1, 3, 2).reshape(g * 512, n)

def pack4(w):
    words, scales = pack_weight(w, "e2m1")
    return words.reshape(words.shape[0], 128, -1), scales


def unpack4(words, scales):
    return unpack_weight(words.reshape(words.shape[0], 128, -1, 2), scales, "e2m1")


B, S, D, H, QB = 1, 1024, 1024, 8, 512
HD = D // H
HALF = HD // 2


def rope_cache():
    inv_freq = 1.0 / (10000.0 ** (np.arange(HALF) / max(HALF, 1)))
    ang = np.arange(S)[:, None] * inv_freq[None, :]
    return np.cos(ang)[None, None], np.sin(ang)[None, None]


def apply_rope(u, cos, sin):
    u1, u2 = u[..., :HALF], u[..., HALF:]
    return np.concatenate([u1 * cos - u2 * sin, u1 * sin + u2 * cos], axis=-1)


def setup_inputs():
    s = mx_kscale(D)
    x = bf(np.random.standard_normal((B, S, D)) * s)
    Wq = np.random.standard_normal((2 * D, D)) / np.sqrt(D) / s[None, :]
    bq = bf(np.random.standard_normal(2 * D) * 0.2)
    Wk = np.random.standard_normal((2 * D, D)) / np.sqrt(D) / s[None, :]
    bk = bf(np.random.standard_normal(2 * D) * 0.2)
    Wq_words, Wq_scales = pack4(np.ascontiguousarray(Wq.T))
    Wk_words, Wk_scales = pack4(np.ascontiguousarray(Wk.T))
    return {"x": x,
            "Wq_words": Wq_words, "Wq_scales": Wq_scales,
            "bq": bq,
            "Wk_words": Wk_words, "Wk_scales": Wk_scales,
            "bk": bk}


def reference(x, Wq_words, Wq_scales, bq, Wk_words, Wk_scales, bk):
    xq = mxq(f64(x), 2, "e5m2")
    q = ((xq @ unpack4(Wq_words, Wq_scales)) + f64(bq)).reshape(B, S, H, 2 * HD).transpose(0, 2, 1, 3)
    k = ((xq @ unpack4(Wk_words, Wk_scales)) + f64(bk)).reshape(B, S, H, 2 * HD).transpose(0, 2, 1, 3)
    cos, sin = rope_cache()
    q1, q2 = apply_rope(q[..., :HD], cos, sin), apply_rope(q[..., HD:], cos, sin)
    k1, k2 = apply_rope(k[..., :HD], cos, sin), apply_rope(k[..., HD:], cos, sin)
    return q1, q2, k1, k2

@@ -1,0 +1,296 @@
+from contextlib import ExitStack
+
+import concourse.mybir as mybir
+from concourse.masks import make_identity
+
+F32 = mybir.dt.float32
+BF16 = mybir.dt.bfloat16
+I32 = mybir.dt.int32
+U32 = mybir.dt.uint32
+U8 = mybir.dt.uint8
+E5X4 = mybir.dt.float8_e5m2_x4
+E2X4 = mybir.dt.float4_e2m1fn_x4
+ACT = mybir.ActivationFunctionType
+ALU = mybir.AluOpType
+
+FLOPS = 2 * 1024 * 1024 * 4096
+
+P = 128
+TWO_PI = 6.283185307179586
+HALF_PI = 1.5707963267948966
+C1 = int(TWO_PI * 8192.0) / 8192.0
+C2 = int((TWO_PI - C1) * 536870912.0) / 536870912.0
+C3 = TWO_PI - C1 - C2
+
+
+def tile_differentialselfattention_pa_kernel(
+    tc, x, Wq_words, Wq_scales, bq, Wk_words, Wk_scales, bk, out_0, out_1, out_2, out_3
+):
+    nc = tc.nc
+    outs = (out_0, out_1, out_2, out_3)
+    words_in = (Wq_words, Wk_words)
+    scales_in = (Wq_scales, Wk_scales)
+    bias_in = (bq, bk)
+
+    with ExitStack() as ctx:
+        const = ctx.enter_context(tc.tile_pool(name="const", bufs=1))
+        ut_pool = ctx.enter_context(tc.tile_pool(name="ut", bufs=4))
+        prod_pool = ctx.enter_context(tc.tile_pool(name="prod", bufs=3))
+        res_pool = ctx.enter_context(tc.tile_pool(name="res", bufs=4))
+        psum_m = ctx.enter_context(tc.psum_pool(name="psm", bufs=4))
+        psum_o = ctx.enter_context(tc.psum_pool(name="pso", bufs=4))
+        ctx.enter_context(tc.manual_schedule())
+
+        x_sb = [const.tile([P, 1024], BF16, name="x%d" % j) for j in range(8)]
+        xg = [const.tile([P, 2, 2048], BF16, name="xg%d" % h, align_bytes=64) for h in range(2)]
+        xc = [const.tile([P, 2, 512], U32, name="xc%d" % h, align_bytes=64) for h in range(2)]
+        xs = [const.tile([P, 2, 512], U8, name="xs%d" % h, align_bytes=64) for h in range(2)]
+        w_sb = [
+            [const.tile([P, 2, 2048], U8, name="w%d%d" % (w, c), align_bytes=64) for c in range(2)]
+            for w in range(2)
+        ]
+        plane = [const.tile([P, 2, 2048], U8, name="pl%d" % w, align_bytes=64) for w in range(2)]
+        ident = const.tile([P, P], F32, name="ident")
+        bias_rows = const.tile([P, P], BF16, name="bias_rows")
+        bias_rows32 = const.tile([P, P], F32, name="bias_rows32")
+        bias_col = const.tile([P, 32], F32, name="bias_col")
+        tok_i = const.tile([P, 8, 1], I32, name="tok_i")
+        tok = const.tile([P, 8, 1], F32, name="tok")
+        freq = const.tile([P, 1, 64], F32, name="freq")
+        table = const.tile([P, 8, 192], F32, name="table")
+        zero1 = const.tile([P, 1], F32, name="zero1")
+        junk1 = const.tile([P, 1], F32, name="junk1")
+
+        x_view = x[0].rearrange("(p j) k -> p j k", j=8)
+
+        def load_x(j):
+            nc.sync.dma_start(out=x_sb[j][:], in_=x_view[:, j, :])
+
+        def load_scales(w):
+            for q in range(4):
+                nc.sync.dma_start(
+                    out=plane[w][32 * q : 32 * q + 4, :, :].bitcast(I32),
+                    in_=scales_in[w][:, 4 * q : 4 * q + 4, :].rearrange("g r n -> r g n").bitcast(I32),
+                )
+
+        def load_words(w, c):
+            for g in range(2):
+                nc.sync.dma_start(
+                    out=w_sb[w][c][:, g, :].bitcast(I32),
+                    in_=words_in[w][g][:, 2048 * c : 2048 * (c + 1)].bitcast(I32),
+                )
+
+        for j in range(4):
+            load_x(j)
+
+        nc.gpsimd.iota(tok_i[:].rearrange("p j o -> p (j o)"), pattern=[[1, 8]], base=0, channel_multiplier=8)
+        make_identity(nc, ident[:])
+        nc.gpsimd.memset(bias_rows[:], 0.0)
+        for w in range(2):
+            nc.gpsimd.memset(plane[w][:].bitcast(F32), 0.0)
+
+        nc.vector.memset(zero1[:], 0.0)
+        nc.scalar.activation(out=junk1[:], in_=zero1[:], func=ACT.Sin)
+
+        for w in range(2):
+            nc.sync.dma_start(
+                out=bias_rows[16 * w : 16 * w + 16, :], in_=bias_in[w].rearrange("(r c) -> r c", c=P)
+            )
+        load_scales(0)
+        load_words(0, 0)
+        for j in range(4, 8):
+            load_x(j)
+        load_words(0, 1)
+        load_scales(1)
+        load_words(1, 0)
+        load_words(1, 1)
+
+        nc.vector.tensor_copy(out=tok[:], in_=tok_i[:])
+        nc.vector.memset(freq[:, :, 0:1], 1.0)
+        for m in range(6):
+            n = 2**m
+            nc.vector.tensor_scalar_mul(
+                out=freq[:, :, n : 2 * n], in0=freq[:, :, 0:n], scalar1=10000.0 ** (-n / 64.0)
+            )
+
+        trig = {}
+
+        def table_angles(h):
+            js = slice(4 * h, 4 * h + 4)
+            th = const.tile([P, 4, 64], F32, name="th%d" % h)
+            ki = const.tile([P, 4, 64], I32, name="ki%d" % h)
+            r1 = const.tile([P, 4, 64], F32, name="r1%d" % h)
+            r2 = const.tile([P, 4, 64], F32, name="r2%d" % h)
+            psi = const.tile([P, 4, 64], F32, name="psi%d" % h)
+            nc.vector.tensor_tensor(
+                out=th[:],
+                in0=tok[:, js, :].to_broadcast([P, 4, 64]),
+                in1=freq[:].to_broadcast([P, 4, 64]),
+                op=ALU.mult,
+            )
+            nc.vector.tensor_scalar(
+                out=ki[:], in0=th[:], scalar1=1.0 / TWO_PI, scalar2=0.25, op0=ALU.mult, op1=ALU.add
+            )
+            nc.vector.scalar_tensor_tensor(out=r1[:], in0=ki[:], scalar=-C1, in1=th[:], op0=ALU.mult, op1=ALU.add)
+            nc.vector.scalar_tensor_tensor(out=r2[:], in0=ki[:], scalar=-C2, in1=r1[:], op0=ALU.mult, op1=ALU.add)
+            nc.vector.scalar_tensor_tensor(out=psi[:], in0=ki[:], scalar=-C3, in1=r2[:], op0=ALU.mult, op1=ALU.add)
+            trig[h] = psi
+
+        def table_trig(h):
+            psi = trig[h]
+            ab = const.tile([P, 4, 64], F32, name="ab%d" % h)
+            sa = const.tile([P, 4, 64], F32, name="sa%d" % h)
+            sb = const.tile([P, 4, 64], F32, name="sb%d" % h)
+            nc.scalar.activation(out=ab[:], in_=psi[:], func=ACT.Abs, scale=0.5)
+            nc.scalar.activation(out=sa[:], in_=psi[:], func=ACT.Sin, scale=0.5)
+            nc.scalar.activation(out=sb[:], in_=ab[:], func=ACT.Sin, bias=HALF_PI, scale=-1.0)
+            trig[h] = (sa, sb)
+
+        def table_fill(h):
+            js = slice(4 * h, 4 * h + 4)
+            sa, sb = trig[h]
+            aa = const.tile([P, 4, 64], F32, name="aa%d" % h)
+            nc.vector.scalar_tensor_tensor(
+                out=table[:, js, 128:192], in0=sa[:], scalar=2.0, in1=sb[:], op0=ALU.mult, op1=ALU.mult
+            )
+            nc.vector.scalar_tensor_tensor(
+                out=table[:, js, 0:64], in0=sa[:], scalar=-2.0, in1=sb[:], op0=ALU.mult, op1=ALU.mult
+            )
+            nc.vector.scalar_tensor_tensor(out=aa[:], in0=sa[:], scalar=-2.0, in1=sa[:], op0=ALU.mult, op1=ALU.mult)
+            nc.vector.tensor_scalar_add(out=table[:, js, 64:128], in0=aa[:], scalar1=1.0)
+
+        xt_tiles = {}
+
+        def xprep_transpose(j):
+            xt = psum_o.tile([P, 4, P], F32, name="xt", tag="o")
+            xw = x_sb[j][:].bitcast(F32)
+            for g in range(2):
+                for u in range(2):
+                    nc.tensor.transpose(xt[:, 2 * g + u, :], xw[:, 256 * g + u : 256 * (g + 1) : 2], ident[:])
+            xt_tiles[j] = xt
+
+        def xprep_copy(j):
+            h, jj = j // 4, j % 4
+            nc.scalar.copy(
+                out=xg[h][:].bitcast(F32).rearrange("p g (t u) -> p g t u", u=2)[:, :, P * jj : P * (jj + 1), :],
+                in_=xt_tiles[j][:].rearrange("p (g u) t -> p g t u", u=2),
+            )
+
+        def xquant(j):
+            h, jj = j // 4, j % 4
+            for g in range(2):
+                nc.vector.quantize_mx(
+                    out=xc[h][:, g, P * jj : P * (jj + 1)].bitcast(E5X4),
+                    scales=xs[h][:, g, P * jj : P * (jj + 1)],
+                    in_=xg[h][:, g, 512 * jj : 512 * (jj + 1)],
+                )
+
+        table_angles(0)
+        table_trig(0)
+        table_angles(1)
+        nc.gpsimd.tensor_copy(out=bias_rows32[:], in_=bias_rows[:])
+        for j in range(4):
+            xprep_transpose(j)
+            xprep_copy(j)
+        table_fill(0)
+        for j in range(4):
+            xquant(j)
+        bias_ps = psum_o.tile([P, P], F32, name="bias_ps", tag="o")
+        nc.tensor.transpose(bias_ps[:], bias_rows32[:], ident[:])
+        nc.scalar.copy(out=bias_col[:], in_=bias_ps[:, 0:32])
+        table_trig(1)
+        table_fill(1)
+
+        live = {}
+
+        def mx(u):
+            h, s = u // 32, u % 32
+            w, sp = s // 16, s % 16
+            c, sl = sp // 8, sp % 8
+            acc = psum_m.tile([P, 512], F32, name="acc", tag="m")
+            for g in range(2):
+                nc.tensor.matmul_mx(
+                    out=acc[:],
+                    lhsT=w_sb[w][c][:, g, 256 * sl : 256 * (sl + 1)].bitcast(E2X4),
+                    lhsT_scale=plane[w][:, g, P * sp : P * (sp + 1)],
+                    rhs=xc[h][:, g, :].bitcast(E5X4),
+                    rhs_scale=xs[h][:, g, :],
+                    start=(g == 0),
+                    stop=(g == 1),
+                )
+            live[("acc", u)] = acc
+
+        def evac(u):
+            s = u % 32
+            ut = ut_pool.tile([P, 512], F32, name="ut", tag="ut")
+            nc.scalar.activation(
+                out=ut[:], in_=live.pop(("acc", u))[:], func=ACT.Identity, bias=bias_col[:, s : s + 1], scale=1.0
+            )
+            live[("ut", u)] = ut
+
+        def tr(u):
+            ut = live.pop(("ut", u))
+            o = psum_o.tile([P, 4, 2, 64], F32, name="o", tag="o")
+            for jj in range(4):
+                nc.tensor.transpose(
+                    o[:, jj, :, :].rearrange("p h i -> p (h i)"), ut[:, P * jj : P * (jj + 1)], ident[:]
+                )
+            live[("o", u)] = o
+
+        def mul(u):
+            h = u // 32
+            js = slice(4 * h, 4 * h + 4)
+            o = live.pop(("o", u))
+            x0 = prod_pool.tile([P, 4, 2, 64], F32, name="x0", tag="x0")
+            x1 = prod_pool.tile([P, 4, 2, 64], F32, name="x1", tag="x1")
+            nc.vector.tensor_tensor(
+                out=x0[:],
+                in0=o[:, :, 0:1, :].to_broadcast([P, 4, 2, 64]),
+                in1=table[:, js, 64:192].rearrange("p j (h i) -> p j h i", h=2),
+                op=ALU.mult,
+            )
+            nc.vector.tensor_tensor(
+                out=x1[:],
+                in0=o[:, :, 1:2, :].to_broadcast([P, 4, 2, 64]),
+                in1=table[:, js, 0:128].rearrange("p j (h i) -> p j h i", h=2),
+                op=ALU.mult,
+            )
+            live[("x", u)] = (x0, x1)
+
+        def add_store(u):
+            h, s = u // 32, u % 32
+            w, sp = s // 16, s % 16
+            head, part = sp // 2, sp % 2
+            x0, x1 = live.pop(("x", u))
+            r = res_pool.tile([P, 4, P], F32, name="r", tag="r")
+            nc.gpsimd.tensor_tensor(
+                out=r[:].rearrange("p j d -> p (j d)"),
+                in0=x0[:].rearrange("p j h i -> p (j h i)"),
+                in1=x1[:].rearrange("p j h i -> p (j h i)"),
+                op=ALU.add,
+            )
+            nc.sync.dma_start(
+                out=outs[2 * w + part][0, head].rearrange("(p j) d -> p j d", j=8)[:, 4 * h : 4 * h + 4, :],
+                in_=r[:],
+            )
+
+        for k in range(33):
+            if k < 32:
+                mx(2 * k)
+                mx(2 * k + 1)
+                evac(2 * k)
+                evac(2 * k + 1)
+            if k >= 1:
+                tr(2 * k - 2)
+                tr(2 * k - 1)
+            if 4 <= k < 8:
+                xprep_transpose(k)
+                xprep_copy(k)
+            if k >= 1:
+                mul(2 * k - 2)
+                mul(2 * k - 1)
+            if 5 <= k < 9:
+                xquant(k - 1)
+            if k >= 1:
+                add_store(2 * k - 2)
+                add_store(2 * k - 1)

@@ -17,10 +17,21 @@ FLOPS = 2 * 1024 * 1024 * 4096
 
 P = 128
 TWO_PI = 6.283185307179586
-HALF_PI = 1.5707963267948966
+QUARTER_PI = 0.7853981633974483
+SQRT2 = 1.4142135623730951
 C1 = int(TWO_PI * 8192.0) / 8192.0
-C2 = int((TWO_PI - C1) * 536870912.0) / 536870912.0
-C3 = TWO_PI - C1 - C2
+C2 = TWO_PI - C1
+B_PERIOD = 4
+
+
+def is_b(u):
+    return u % 4 == 3 and 11 <= u < 63
+
+
+def units(k):
+    if 0 <= k < 32:
+        return [2 * k, 2 * k + 1]
+    return []
 
 
 def tile_differentialselfattention_pa_kernel(
@@ -35,14 +46,15 @@ def tile_differentialselfattention_pa_kernel(
     with ExitStack() as ctx:
         const = ctx.enter_context(tc.tile_pool(name="const", bufs=1))
         ut_pool = ctx.enter_context(tc.tile_pool(name="ut", bufs=4))
-        prod_pool = ctx.enter_context(tc.tile_pool(name="prod", bufs=3))
-        res_pool = ctx.enter_context(tc.tile_pool(name="res", bufs=4))
+        prod_pool = ctx.enter_context(tc.tile_pool(name="prod", bufs=4))
+        z_pool = ctx.enter_context(tc.tile_pool(name="zp", bufs=2))
+        res_pool = ctx.enter_context(tc.tile_pool(name="res", bufs=8))
         psum_m = ctx.enter_context(tc.psum_pool(name="psm", bufs=4))
         psum_o = ctx.enter_context(tc.psum_pool(name="pso", bufs=4))
         ctx.enter_context(tc.manual_schedule())
 
         x_sb = [const.tile([P, 1024], BF16, name="x%d" % j) for j in range(8)]
-        xg = [const.tile([P, 2, 2048], BF16, name="xg%d" % h, align_bytes=64) for h in range(2)]
+        xg = [const.tile([P, 2, 512], BF16, name="xg%d" % j, align_bytes=64) for j in range(8)]
         xc = [const.tile([P, 2, 512], U32, name="xc%d" % h, align_bytes=64) for h in range(2)]
         xs = [const.tile([P, 2, 512], U8, name="xs%d" % h, align_bytes=64) for h in range(2)]
         w_sb = [
@@ -51,6 +63,7 @@ def tile_differentialselfattention_pa_kernel(
         ]
         plane = [const.tile([P, 2, 2048], U8, name="pl%d" % w, align_bytes=64) for w in range(2)]
         ident = const.tile([P, P], F32, name="ident")
+        perm = const.tile([P, P], F32, name="perm")
         bias_rows = const.tile([P, P], BF16, name="bias_rows")
         bias_rows32 = const.tile([P, P], F32, name="bias_rows32")
         bias_col = const.tile([P, 32], F32, name="bias_col")
@@ -58,6 +71,10 @@ def tile_differentialselfattention_pa_kernel(
         tok = const.tile([P, 8, 1], F32, name="tok")
         freq = const.tile([P, 1, 64], F32, name="freq")
         table = const.tile([P, 8, 192], F32, name="table")
+        cc_a = [const.tile([P, 4, 2, 64], F32, name="cca%d" % h) for h in range(2)]
+        ss_a = [const.tile([P, 4, 2, 64], F32, name="ssa%d" % h) for h in range(2)]
+        cc_b = [const.tile([P, 512], F32, name="ccb%d" % h) for h in range(2)]
+        ss_b = [const.tile([P, 512], F32, name="ssb%d" % h) for h in range(2)]
         zero1 = const.tile([P, 1], F32, name="zero1")
         junk1 = const.tile([P, 1], F32, name="junk1")
 
@@ -74,36 +91,32 @@ def tile_differentialselfattention_pa_kernel(
                 )
 
         def load_words(w, c):
-            for g in range(2):
-                nc.sync.dma_start(
-                    out=w_sb[w][c][:, g, :].bitcast(I32),
-                    in_=words_in[w][g][:, 2048 * c : 2048 * (c + 1)].bitcast(I32),
-                )
+            nc.sync.dma_start(
+                out=w_sb[w][c][:].bitcast(I32),
+                in_=words_in[w][:, :, 2048 * c : 2048 * (c + 1)].rearrange("g p n -> p g n").bitcast(I32),
+            )
 
         for j in range(4):
             load_x(j)
+        load_words(0, 0)
 
         nc.gpsimd.iota(tok_i[:].rearrange("p j o -> p (j o)"), pattern=[[1, 8]], base=0, channel_multiplier=8)
+        nc.gpsimd.memset(plane[0][:].bitcast(F32), 0.0)
+        load_scales(0)
         make_identity(nc, ident[:])
-        nc.gpsimd.memset(bias_rows[:], 0.0)
+        nc.gpsimd.memset(bias_rows[32:64, :], 0.0)
+        nc.gpsimd.memset(bias_rows[64:128, :], 0.0)
         for w in range(2):
-            nc.gpsimd.memset(plane[w][:].bitcast(F32), 0.0)
-
-        nc.vector.memset(zero1[:], 0.0)
-        nc.scalar.activation(out=junk1[:], in_=zero1[:], func=ACT.Sin)
-
-        for w in range(2):
-            nc.sync.dma_start(
+            nc.gpsimd.dma_start(
                 out=bias_rows[16 * w : 16 * w + 16, :], in_=bias_in[w].rearrange("(r c) -> r c", c=P)
             )
-        load_scales(0)
-        load_words(0, 0)
+
         for j in range(4, 8):
             load_x(j)
         load_words(0, 1)
-        load_scales(1)
-        load_words(1, 0)
-        load_words(1, 1)
+
+        nc.vector.memset(zero1[:], 0.0)
+        nc.scalar.activation(out=junk1[:], in_=zero1[:], func=ACT.Sin)
 
         nc.vector.tensor_copy(out=tok[:], in_=tok_i[:])
         nc.vector.memset(freq[:, :, 0:1], 1.0)
@@ -113,15 +126,17 @@ def tile_differentialselfattention_pa_kernel(
                 out=freq[:, :, n : 2 * n], in0=freq[:, :, 0:n], scalar1=10000.0 ** (-n / 64.0)
             )
 
-        trig = {}
+        psi = [const.tile([P, 4, 64], F32, name="psi%d" % h) for h in range(2)]
+        sin_c = [const.tile([P, 4, 64], F32, name="sinc%d" % h) for h in range(2)]
+        sin_s = [const.tile([P, 4, 64], F32, name="sins%d" % h) for h in range(2)]
+        q_c = [const.tile([P, 4, 1, 64], F32, name="qc%d" % h) for h in range(2)]
+        q_s = [const.tile([P, 4, 1, 64], F32, name="qs%d" % h) for h in range(2)]
 
         def table_angles(h):
             js = slice(4 * h, 4 * h + 4)
             th = const.tile([P, 4, 64], F32, name="th%d" % h)
             ki = const.tile([P, 4, 64], I32, name="ki%d" % h)
             r1 = const.tile([P, 4, 64], F32, name="r1%d" % h)
-            r2 = const.tile([P, 4, 64], F32, name="r2%d" % h)
-            psi = const.tile([P, 4, 64], F32, name="psi%d" % h)
             nc.vector.tensor_tensor(
                 out=th[:],
                 in0=tok[:, js, :].to_broadcast([P, 4, 64]),
@@ -129,35 +144,61 @@ def tile_differentialselfattention_pa_kernel(
                 op=ALU.mult,
             )
             nc.vector.tensor_scalar(
-                out=ki[:], in0=th[:], scalar1=1.0 / TWO_PI, scalar2=0.25, op0=ALU.mult, op1=ALU.add
+                out=ki[:], in0=th[:], scalar1=1.0 / TWO_PI, scalar2=0.125, op0=ALU.mult, op1=ALU.add
             )
             nc.vector.scalar_tensor_tensor(out=r1[:], in0=ki[:], scalar=-C1, in1=th[:], op0=ALU.mult, op1=ALU.add)
-            nc.vector.scalar_tensor_tensor(out=r2[:], in0=ki[:], scalar=-C2, in1=r1[:], op0=ALU.mult, op1=ALU.add)
-            nc.vector.scalar_tensor_tensor(out=psi[:], in0=ki[:], scalar=-C3, in1=r2[:], op0=ALU.mult, op1=ALU.add)
-            trig[h] = psi
+            nc.vector.scalar_tensor_tensor(
+                out=psi[h][:], in0=ki[:], scalar=-C2, in1=r1[:], op0=ALU.mult, op1=ALU.add
+            )
 
-        def table_trig(h):
-            psi = trig[h]
-            ab = const.tile([P, 4, 64], F32, name="ab%d" % h)
-            sa = const.tile([P, 4, 64], F32, name="sa%d" % h)
-            sb = const.tile([P, 4, 64], F32, name="sb%d" % h)
-            nc.scalar.activation(out=ab[:], in_=psi[:], func=ACT.Abs, scale=0.5)
-            nc.scalar.activation(out=sa[:], in_=psi[:], func=ACT.Sin, scale=0.5)
-            nc.scalar.activation(out=sb[:], in_=ab[:], func=ACT.Sin, bias=HALF_PI, scale=-1.0)
-            trig[h] = (sa, sb)
+        def trig_ops(h):
+            return [
+                lambda: nc.scalar.activation(out=sin_c[h][:], in_=psi[h][:], func=ACT.Sin, scale=0.5),
+                lambda: nc.scalar.activation(
+                    out=sin_s[h][:], in_=psi[h][:], func=ACT.Sin, bias=-QUARTER_PI, scale=0.5
+                ),
+                lambda: nc.scalar.activation(
+                    out=q_c[h][:, :, 0, :], in_=sin_c[h][:], func=ACT.Square, scale=SQRT2
+                ),
+                lambda: nc.scalar.activation(
+                    out=q_s[h][:, :, 0, :], in_=sin_s[h][:], func=ACT.Square, scale=SQRT2
+                ),
+            ]
 
-        def table_fill(h):
+        def affine(on_gpsimd, out, in_, sign):
+            if on_gpsimd:
+                nc.gpsimd.tensor_scalar(
+                    out=out, in0=in_, scalar1=-sign, scalar2=sign, op0=ALU.mult, op1=ALU.add
+                )
+            else:
+                nc.scalar.activation(out=out, in_=in_, func=ACT.Identity, bias=sign, scale=-sign)
+
+        def fill_ops(h, g):
             js = slice(4 * h, 4 * h + 4)
-            sa, sb = trig[h]
-            aa = const.tile([P, 4, 64], F32, name="aa%d" % h)
-            nc.vector.scalar_tensor_tensor(
-                out=table[:, js, 128:192], in0=sa[:], scalar=2.0, in1=sb[:], op0=ALU.mult, op1=ALU.mult
-            )
-            nc.vector.scalar_tensor_tensor(
-                out=table[:, js, 0:64], in0=sa[:], scalar=-2.0, in1=sb[:], op0=ALU.mult, op1=ALU.mult
-            )
-            nc.vector.scalar_tensor_tensor(out=aa[:], in0=sa[:], scalar=-2.0, in1=sa[:], op0=ALU.mult, op1=ALU.mult)
-            nc.vector.tensor_scalar_add(out=table[:, js, 64:128], in0=aa[:], scalar1=1.0)
+            return [
+                lambda: affine(g, table[:, js, 64:128], q_c[h][:, :, 0, :], 1.0),
+                lambda: affine(g, table[:, js, 128:192], q_s[h][:, :, 0, :], 1.0),
+                lambda: affine(g, table[:, js, 0:64], q_s[h][:, :, 0, :], -1.0),
+                lambda: affine(g, cc_a[h][:], q_c[h][:].to_broadcast([P, 4, 2, 64]), 1.0),
+                lambda: affine(g, ss_a[h][:, :, 0, :], q_s[h][:, :, 0, :], 1.0),
+                lambda: affine(g, ss_a[h][:, :, 1, :], q_s[h][:, :, 0, :], -1.0),
+            ]
+
+        tb_ps = {}
+
+        def tableb_transpose(h):
+            cps = psum_o.tile([P, 4, P], F32, name="cps", tag="o")
+            sps = psum_o.tile([P, 4, P], F32, name="sps", tag="o")
+            for jj in range(4):
+                nc.tensor.transpose(cps[:, jj, :], cc_a[h][:, jj, :, :].rearrange("p k i -> p (k i)"), ident[:])
+            for jj in range(4):
+                nc.tensor.transpose(sps[:, jj, :], ss_a[h][:, jj, :, :].rearrange("p k i -> p (k i)"), ident[:])
+            tb_ps[h] = (cps, sps)
+
+        def tableb_copy(h):
+            cps, sps = tb_ps[h]
+            nc.scalar.copy(out=cc_b[h][:], in_=cps[:].rearrange("p j t -> p (j t)"))
+            nc.scalar.copy(out=ss_b[h][:], in_=sps[:].rearrange("p j t -> p (j t)"))
 
         xt_tiles = {}
 
@@ -170,9 +211,8 @@ def tile_differentialselfattention_pa_kernel(
             xt_tiles[j] = xt
 
         def xprep_copy(j):
-            h, jj = j // 4, j % 4
             nc.scalar.copy(
-                out=xg[h][:].bitcast(F32).rearrange("p g (t u) -> p g t u", u=2)[:, :, P * jj : P * (jj + 1), :],
+                out=xg[j][:].bitcast(F32).rearrange("p g (t u) -> p g t u", u=2),
                 in_=xt_tiles[j][:].rearrange("p (g u) t -> p g t u", u=2),
             )
 
@@ -182,24 +222,34 @@ def tile_differentialselfattention_pa_kernel(
                 nc.vector.quantize_mx(
                     out=xc[h][:, g, P * jj : P * (jj + 1)].bitcast(E5X4),
                     scales=xs[h][:, g, P * jj : P * (jj + 1)],
-                    in_=xg[h][:, g, 512 * jj : 512 * (jj + 1)],
+                    in_=xg[j][:, g, :],
                 )
 
         table_angles(0)
-        table_trig(0)
         table_angles(1)
-        nc.gpsimd.tensor_copy(out=bias_rows32[:], in_=bias_rows[:])
+        for op in trig_ops(0):
+            op()
+        fill0 = fill_ops(0, True)
+        for op in fill0[0:3]:
+            op()
+        nc.gpsimd.tensor_scalar(
+            out=bias_rows32[:], in0=bias_rows[:], scalar1=1.0, scalar2=0.0, op0=ALU.mult, op1=ALU.add
+        )
+        nc.gpsimd.memset(plane[1][:].bitcast(F32), 0.0)
+        load_scales(1)
+        load_words(1, 0)
+        load_words(1, 1)
+        nc.gpsimd.tensor_copy(out=perm[:, 0:64], in_=ident[:, 64:128])
+        nc.gpsimd.tensor_copy(out=perm[:, 64:128], in_=ident[:, 0:64])
+        for op in fill0[3:6]:
+            op()
         for j in range(4):
             xprep_transpose(j)
             xprep_copy(j)
-        table_fill(0)
-        for j in range(4):
             xquant(j)
         bias_ps = psum_o.tile([P, P], F32, name="bias_ps", tag="o")
         nc.tensor.transpose(bias_ps[:], bias_rows32[:], ident[:])
         nc.scalar.copy(out=bias_col[:], in_=bias_ps[:, 0:32])
-        table_trig(1)
-        table_fill(1)
 
         live = {}
 
@@ -257,40 +307,110 @@ def tile_differentialselfattention_pa_kernel(
             )
             live[("x", u)] = (x0, x1)
 
-        def add_store(u):
+        def store(u, r):
             h, s = u // 32, u % 32
             w, sp = s // 16, s % 16
             head, part = sp // 2, sp % 2
-            x0, x1 = live.pop(("x", u))
-            r = res_pool.tile([P, 4, P], F32, name="r", tag="r")
-            nc.gpsimd.tensor_tensor(
-                out=r[:].rearrange("p j d -> p (j d)"),
-                in0=x0[:].rearrange("p j h i -> p (j h i)"),
-                in1=x1[:].rearrange("p j h i -> p (j h i)"),
-                op=ALU.add,
-            )
             nc.sync.dma_start(
                 out=outs[2 * w + part][0, head].rearrange("(p j) d -> p j d", j=8)[:, 4 * h : 4 * h + 4, :],
                 in_=r[:],
             )
 
-        for k in range(33):
-            if k < 32:
-                mx(2 * k)
-                mx(2 * k + 1)
-                evac(2 * k)
-                evac(2 * k + 1)
-            if k >= 1:
-                tr(2 * k - 2)
-                tr(2 * k - 1)
-            if 4 <= k < 8:
-                xprep_transpose(k)
-                xprep_copy(k)
-            if k >= 1:
-                mul(2 * k - 2)
-                mul(2 * k - 1)
-            if 5 <= k < 9:
-                xquant(k - 1)
-            if k >= 1:
-                add_store(2 * k - 2)
-                add_store(2 * k - 1)
+        def add_store(u, on_vector):
+            x0, x1 = live.pop(("x", u))
+            r = res_pool.tile([P, 4, P], F32, name="r", tag="r")
+            eng = nc.vector if on_vector else nc.gpsimd
+            eng.tensor_tensor(
+                out=r[:].rearrange("p j d -> p (j d)"),
+                in0=x0[:].rearrange("p j h i -> p (j h i)"),
+                in1=x1[:].rearrange("p j h i -> p (j h i)"),
+                op=ALU.add,
+            )
+            store(u, r)
+
+        def zmul(u):
+            h, s = u // 32, u % 32
+            acc = live.pop(("acc", u))
+            za = z_pool.tile([P, 512], F32, name="za", tag="za")
+            zb = z_pool.tile([P, 512], F32, name="zb", tag="zb")
+            nc.vector.scalar_tensor_tensor(
+                out=za[:], in0=acc[:], scalar=bias_col[:, s : s + 1], in1=cc_b[h][:], op0=ALU.add, op1=ALU.mult
+            )
+            nc.vector.scalar_tensor_tensor(
+                out=zb[:], in0=acc[:], scalar=bias_col[:, s : s + 1], in1=ss_b[h][:], op0=ALU.add, op1=ALU.mult
+            )
+            live[("z", u)] = (za, zb)
+
+        def tradd(u):
+            za, zb = live.pop(("z", u))
+            ob = psum_o.tile([P, 4, P], F32, name="ob", tag="o")
+            for jj in range(4):
+                cols = slice(P * jj, P * (jj + 1))
+                nc.tensor.matmul(
+                    ob[:, jj, :], lhsT=za[:, cols], rhs=ident[:], start=True, stop=False, is_transpose=True
+                )
+                nc.tensor.matmul(
+                    ob[:, jj, :], lhsT=zb[:, cols], rhs=perm[:], start=False, stop=True, is_transpose=True
+                )
+            live[("ob", u)] = ob
+
+        def copy_store(u):
+            ob = live.pop(("ob", u))
+            r = res_pool.tile([P, 4, P], F32, name="r", tag="r")
+            nc.scalar.copy(out=r[:], in_=ob[:])
+            store(u, r)
+
+        trig1 = trig_ops(1)
+        fill1 = fill_ops(1, False)
+        scalar_extra = {
+            4: trig1[0:2],
+            5: trig1[2:4],
+            6: fill1[0:2],
+            7: fill1[2:4],
+            8: fill1[4:6],
+        }
+
+        for k in range(37):
+            if k > 1:
+                for u in units(k):
+                    mx(u)
+            for u in units(k - 1):
+                if not is_b(u):
+                    tr(u)
+            for u in units(k - 2):
+                if is_b(u):
+                    tradd(u)
+            if k == 3:
+                tableb_transpose(0)
+            if k == 12:
+                tableb_transpose(1)
+            if 8 <= k < 8 + 4:
+                xprep_transpose(k - 8 + 4)
+            if k <= 1:
+                for u in units(k):
+                    mx(u)
+            for u in units(k):
+                if not is_b(u):
+                    evac(u)
+            for u in units(k - 2):
+                if is_b(u):
+                    copy_store(u)
+            if k == 3:
+                tableb_copy(0)
+            if k == 12:
+                tableb_copy(1)
+            if 8 <= k < 8 + 4:
+                xprep_copy(k - 8 + 4)
+            for op in scalar_extra.get(k, []):
+                op()
+            for u in units(k - 0):
+                if is_b(u):
+                    zmul(u)
+            for u in units(k - 1):
+                if not is_b(u):
+                    mul(u)
+            if 8 + 1 <= k < 8 + 5:
+                xquant(k - 8 + 3)
+            for u in units(k - 1):
+                if not is_b(u):
+                    add_store(u, u >= 62)

@@ -70,11 +70,10 @@ def tile_differentialselfattention_pa_kernel(
         tok_i = const.tile([P, 8, 1], I32, name="tok_i")
         tok = const.tile([P, 8, 1], F32, name="tok")
         freq = const.tile([P, 1, 64], F32, name="freq")
-        table = const.tile([P, 8, 192], F32, name="table")
+        table = const.tile([P, 8, 256], F32, name="table")
         cc_a = [const.tile([P, 4, 2, 64], F32, name="cca%d" % h) for h in range(2)]
         ss_a = [const.tile([P, 4, 2, 64], F32, name="ssa%d" % h) for h in range(2)]
-        cc_b = [const.tile([P, 512], F32, name="ccb%d" % h) for h in range(2)]
-        ss_b = [const.tile([P, 512], F32, name="ssb%d" % h) for h in range(2)]
+        cs_b = [const.tile([P, 2, 512], F32, name="csb%d" % h) for h in range(2)]
         zero1 = const.tile([P, 1], F32, name="zero1")
         junk1 = const.tile([P, 1], F32, name="junk1")
 
@@ -176,9 +175,14 @@ def tile_differentialselfattention_pa_kernel(
         def fill_ops(h, g):
             js = slice(4 * h, 4 * h + 4)
             return [
-                lambda: affine(g, table[:, js, 64:128], q_c[h][:, :, 0, :], 1.0),
-                lambda: affine(g, table[:, js, 128:192], q_s[h][:, :, 0, :], 1.0),
-                lambda: affine(g, table[:, js, 0:64], q_s[h][:, :, 0, :], -1.0),
+                lambda: affine(
+                    g,
+                    table[:, js, :].rearrange("p j (k i) -> p j k i", i=64)[:, :, 0:4:3, :],
+                    q_c[h][:].to_broadcast([P, 4, 2, 64]),
+                    1.0,
+                ),
+                lambda: affine(g, table[:, js, 64:128], q_s[h][:, :, 0, :], 1.0),
+                lambda: affine(g, table[:, js, 128:192], q_s[h][:, :, 0, :], -1.0),
                 lambda: affine(g, cc_a[h][:], q_c[h][:].to_broadcast([P, 4, 2, 64]), 1.0),
                 lambda: affine(g, ss_a[h][:, :, 0, :], q_s[h][:, :, 0, :], 1.0),
                 lambda: affine(g, ss_a[h][:, :, 1, :], q_s[h][:, :, 0, :], -1.0),
@@ -197,8 +201,8 @@ def tile_differentialselfattention_pa_kernel(
 
         def tableb_copy(h):
             cps, sps = tb_ps[h]
-            nc.scalar.copy(out=cc_b[h][:], in_=cps[:].rearrange("p j t -> p (j t)"))
-            nc.scalar.copy(out=ss_b[h][:], in_=sps[:].rearrange("p j t -> p (j t)"))
+            nc.scalar.copy(out=cs_b[h][:, 0, :], in_=cps[:].rearrange("p j t -> p (j t)"))
+            nc.scalar.copy(out=cs_b[h][:, 1, :], in_=sps[:].rearrange("p j t -> p (j t)"))
 
         xt_tiles = {}
 
@@ -257,10 +261,10 @@ def tile_differentialselfattention_pa_kernel(
             h, s = u // 32, u % 32
             w, sp = s // 16, s % 16
             c, sl = sp // 8, sp % 8
-            acc = psum_m.tile([P, 512], F32, name="acc", tag="m")
+            acc = psum_m.tile([P, 1, 512], F32, name="acc", tag="m")
             for g in range(2):
                 nc.tensor.matmul_mx(
-                    out=acc[:],
+                    out=acc[:, 0, :],
                     lhsT=w_sb[w][c][:, g, 256 * sl : 256 * (sl + 1)].bitcast(E2X4),
                     lhsT_scale=plane[w][:, g, P * sp : P * (sp + 1)],
                     rhs=xc[h][:, g, :].bitcast(E5X4),
@@ -274,16 +278,16 @@ def tile_differentialselfattention_pa_kernel(
             s = u % 32
             ut = ut_pool.tile([P, 512], F32, name="ut", tag="ut")
             nc.scalar.activation(
-                out=ut[:], in_=live.pop(("acc", u))[:], func=ACT.Identity, bias=bias_col[:, s : s + 1], scale=1.0
+                out=ut[:], in_=live.pop(("acc", u))[:, 0, :], func=ACT.Identity, bias=bias_col[:, s : s + 1], scale=1.0
             )
             live[("ut", u)] = ut
 
         def tr(u):
             ut = live.pop(("ut", u))
-            o = psum_o.tile([P, 4, 2, 64], F32, name="o", tag="o")
+            o = psum_o.tile([P, 8, 1, 64], F32, name="o", tag="o")
             for jj in range(4):
                 nc.tensor.transpose(
-                    o[:, jj, :, :].rearrange("p h i -> p (h i)"), ut[:, P * jj : P * (jj + 1)], ident[:]
+                    o[:, 2 * jj : 2 * jj + 2, 0, :].rearrange("p m i -> p (m i)"), ut[:, P * jj : P * (jj + 1)], ident[:]
                 )
             live[("o", u)] = o
 
@@ -291,21 +295,14 @@ def tile_differentialselfattention_pa_kernel(
             h = u // 32
             js = slice(4 * h, 4 * h + 4)
             o = live.pop(("o", u))
-            x0 = prod_pool.tile([P, 4, 2, 64], F32, name="x0", tag="x0")
-            x1 = prod_pool.tile([P, 4, 2, 64], F32, name="x1", tag="x1")
+            xp = prod_pool.tile([P, 8, 2, 64], F32, name="xp", tag="xp")
             nc.vector.tensor_tensor(
-                out=x0[:],
-                in0=o[:, :, 0:1, :].to_broadcast([P, 4, 2, 64]),
-                in1=table[:, js, 64:192].rearrange("p j (h i) -> p j h i", h=2),
+                out=xp[:],
+                in0=o[:].to_broadcast([P, 8, 2, 64]),
+                in1=table[:, js, :].rearrange("p j (w h i) -> p (j w) h i", w=2, h=2),
                 op=ALU.mult,
             )
-            nc.vector.tensor_tensor(
-                out=x1[:],
-                in0=o[:, :, 1:2, :].to_broadcast([P, 4, 2, 64]),
-                in1=table[:, js, 0:128].rearrange("p j (h i) -> p j h i", h=2),
-                op=ALU.mult,
-            )
-            live[("x", u)] = (x0, x1)
+            live[("x", u)] = xp
 
         def store(u, r):
             h, s = u // 32, u % 32
@@ -317,40 +314,36 @@ def tile_differentialselfattention_pa_kernel(
             )
 
         def add_store(u, on_vector):
-            x0, x1 = live.pop(("x", u))
+            xp = live.pop(("x", u))[:].rearrange("p (j w) h i -> p j w (h i)", w=2)
             r = res_pool.tile([P, 4, P], F32, name="r", tag="r")
             eng = nc.vector if on_vector else nc.gpsimd
-            eng.tensor_tensor(
-                out=r[:].rearrange("p j d -> p (j d)"),
-                in0=x0[:].rearrange("p j h i -> p (j h i)"),
-                in1=x1[:].rearrange("p j h i -> p (j h i)"),
-                op=ALU.add,
-            )
+            eng.tensor_tensor(out=r[:], in0=xp[:, :, 0, :], in1=xp[:, :, 1, :], op=ALU.add)
             store(u, r)
 
         def zmul(u):
             h, s = u // 32, u % 32
             acc = live.pop(("acc", u))
-            za = z_pool.tile([P, 512], F32, name="za", tag="za")
-            zb = z_pool.tile([P, 512], F32, name="zb", tag="zb")
+            z = z_pool.tile([P, 2, 512], F32, name="z", tag="z")
             nc.vector.scalar_tensor_tensor(
-                out=za[:], in0=acc[:], scalar=bias_col[:, s : s + 1], in1=cc_b[h][:], op0=ALU.add, op1=ALU.mult
+                out=z[:],
+                in0=acc[:].to_broadcast([P, 2, 512]),
+                scalar=bias_col[:, s : s + 1],
+                in1=cs_b[h][:],
+                op0=ALU.add,
+                op1=ALU.mult,
             )
-            nc.vector.scalar_tensor_tensor(
-                out=zb[:], in0=acc[:], scalar=bias_col[:, s : s + 1], in1=ss_b[h][:], op0=ALU.add, op1=ALU.mult
-            )
-            live[("z", u)] = (za, zb)
+            live[("z", u)] = z
 
         def tradd(u):
-            za, zb = live.pop(("z", u))
+            z = live.pop(("z", u))
             ob = psum_o.tile([P, 4, P], F32, name="ob", tag="o")
             for jj in range(4):
                 cols = slice(P * jj, P * (jj + 1))
                 nc.tensor.matmul(
-                    ob[:, jj, :], lhsT=za[:, cols], rhs=ident[:], start=True, stop=False, is_transpose=True
+                    ob[:, jj, :], lhsT=z[:, 0, cols], rhs=ident[:], start=True, stop=False, is_transpose=True
                 )
                 nc.tensor.matmul(
-                    ob[:, jj, :], lhsT=zb[:, cols], rhs=perm[:], start=False, stop=True, is_transpose=True
+                    ob[:, jj, :], lhsT=z[:, 1, cols], rhs=perm[:], start=False, stop=True, is_transpose=True
                 )
             live[("ob", u)] = ob
 

@@ -106,9 +106,12 @@ def tile_differentialselfattention_pa_kernel(
         nc.gpsimd.memset(bias_rows[32:64, :], 0.0)
         nc.gpsimd.memset(bias_rows[64:128, :], 0.0)
         for w in range(2):
-            nc.gpsimd.dma_start(
+            nc.scalar.dma_start(
                 out=bias_rows[16 * w : 16 * w + 16, :], in_=bias_in[w].rearrange("(r c) -> r c", c=P)
             )
+        nc.gpsimd.memset(plane[1][:].bitcast(F32), 0.0)
+        nc.gpsimd.tensor_copy(out=perm[:, 0:64], in_=ident[:, 64:128])
+        nc.gpsimd.tensor_copy(out=perm[:, 64:128], in_=ident[:, 0:64])
 
         for j in range(4, 8):
             load_x(j)
@@ -231,22 +234,21 @@ def tile_differentialselfattention_pa_kernel(
 
         table_angles(0)
         table_angles(1)
-        for op in trig_ops(0):
-            op()
-        fill0 = fill_ops(0, True)
-        for op in fill0[0:3]:
-            op()
         nc.gpsimd.tensor_scalar(
             out=bias_rows32[:], in0=bias_rows[:], scalar1=1.0, scalar2=0.0, op0=ALU.mult, op1=ALU.add
         )
-        nc.gpsimd.memset(plane[1][:].bitcast(F32), 0.0)
+        for op in trig_ops(0)[0:2]:
+            op()
+        for q, s in ((q_c[0], sin_c[0]), (q_s[0], sin_s[0])):
+            nc.vector.scalar_tensor_tensor(
+                out=q[:, :, 0, :], in0=s[:], scalar=2.0, in1=s[:], op0=ALU.mult, op1=ALU.mult
+            )
+        fill0 = fill_ops(0, True)
+        for op in fill0[0:3]:
+            op()
         load_scales(1)
         load_words(1, 0)
         load_words(1, 1)
-        nc.gpsimd.tensor_copy(out=perm[:, 0:64], in_=ident[:, 64:128])
-        nc.gpsimd.tensor_copy(out=perm[:, 64:128], in_=ident[:, 0:64])
-        for op in fill0[3:6]:
-            op()
         for j in range(4):
             xprep_transpose(j)
             xprep_copy(j)
@@ -355,7 +357,11 @@ def tile_differentialselfattention_pa_kernel(
 
         trig1 = trig_ops(1)
         fill1 = fill_ops(1, False)
+        fill0_b = fill_ops(0, False)
         scalar_extra = {
+            0: fill0_b[3:4],
+            1: fill0_b[4:5],
+            2: fill0_b[5:6],
             4: trig1[0:2],
             5: trig1[2:4],
             6: fill1[0:2],

@@ -54,7 +54,8 @@ def tile_differentialselfattention_pa_kernel(
         ctx.enter_context(tc.manual_schedule())
 
         x_sb = [const.tile([P, 1024], BF16, name="x%d" % j) for j in range(8)]
-        xg = [const.tile([P, 2, 512], BF16, name="xg%d" % j, align_bytes=64) for j in range(8)]
+        xg = [const.tile([P, 2, 512], BF16, name="xg%d" % j, align_bytes=64) for j in range(4)]
+        xg_late = const.tile([P, 2, 4, 512], BF16, name="xg_late", align_bytes=64)
         xc = [const.tile([P, 2, 512], U32, name="xc%d" % h, align_bytes=64) for h in range(2)]
         xs = [const.tile([P, 2, 512], U8, name="xs%d" % h, align_bytes=64) for h in range(2)]
         w_sb = [
@@ -218,8 +219,9 @@ def tile_differentialselfattention_pa_kernel(
             xt_tiles[j] = xt
 
         def xprep_copy(j):
+            dst = xg[j][:] if j < 4 else xg_late[:, :, j - 4, :]
             nc.scalar.copy(
-                out=xg[j][:].bitcast(F32).rearrange("p g (t u) -> p g t u", u=2),
+                out=dst.bitcast(F32).rearrange("p g (t u) -> p g t u", u=2),
                 in_=xt_tiles[j][:].rearrange("p (g u) t -> p g t u", u=2),
             )
 
@@ -231,6 +233,13 @@ def tile_differentialselfattention_pa_kernel(
                     scales=xs[h][:, g, P * jj : P * (jj + 1)],
                     in_=xg[j][:, g, :],
                 )
+
+        def xquant_late():
+            nc.vector.quantize_mx(
+                out=xc[1][:].rearrange("p g c -> p (g c)").bitcast(E5X4),
+                scales=xs[1][:].rearrange("p g c -> p (g c)"),
+                in_=xg_late[:].rearrange("p g j c -> p (g j c)"),
+            )
 
         table_angles(0)
         table_angles(1)
@@ -408,8 +417,8 @@ def tile_differentialselfattention_pa_kernel(
             for u in units(k - 1):
                 if not is_b(u):
                     mul(u)
-            if 8 + 1 <= k < 8 + 5:
-                xquant(k - 8 + 3)
+            if k == 8 + 4:
+                xquant_late()
             for u in units(k - 1):
                 if not is_b(u):
                     add_store(u, u >= 62)

@@ -21,11 +21,23 @@ QUARTER_PI = 0.7853981633974483
 SQRT2 = 1.4142135623730951
 C1 = int(TWO_PI * 8192.0) / 8192.0
 C2 = TWO_PI - C1
-B_PERIOD = 4
+
+WARM0 = 5
+WARMJ = 1
+XK = 8
+TBK0 = 3
+TBK1 = 12
+WIDEQ = True
+MERGE_TO = 0
+VADD_FROM = 62
 
 
-def is_b(u):
-    return u % 4 == 3 and 11 <= u < 63
+def kind(u):
+    if u % 4 == 3 and 11 <= u < 63:
+        return "B"
+    if False:
+        return "C"
+    return "A"
 
 
 def units(k):
@@ -47,6 +59,7 @@ def tile_differentialselfattention_pa_kernel(
         const = ctx.enter_context(tc.tile_pool(name="const", bufs=1))
         ut_pool = ctx.enter_context(tc.tile_pool(name="ut", bufs=4))
         prod_pool = ctx.enter_context(tc.tile_pool(name="prod", bufs=4))
+        half_pool = ctx.enter_context(tc.tile_pool(name="half", bufs=2))
         z_pool = ctx.enter_context(tc.tile_pool(name="zp", bufs=2))
         res_pool = ctx.enter_context(tc.tile_pool(name="res", bufs=8))
         psum_m = ctx.enter_context(tc.psum_pool(name="psm", bufs=4))
@@ -77,6 +90,8 @@ def tile_differentialselfattention_pa_kernel(
         cs_b = [const.tile([P, 2, 512], F32, name="csb%d" % h) for h in range(2)]
         zero1 = const.tile([P, 1], F32, name="zero1")
         junk1 = const.tile([P, 1], F32, name="junk1")
+        idle_words = const.tile([P, 256], F32, name="idle_words")
+        idle_in = idle_words[:].bitcast(BF16)
 
         x_view = x[0].rearrange("(p j) k -> p j k", j=8)
 
@@ -100,6 +115,8 @@ def tile_differentialselfattention_pa_kernel(
             load_x(j)
         load_words(0, 0)
 
+        if WARM0 or WARMJ:
+            nc.vector.memset(idle_words[:], 0.0)
         nc.gpsimd.iota(tok_i[:].rearrange("p j o -> p (j o)"), pattern=[[1, 8]], base=0, channel_multiplier=8)
         nc.gpsimd.memset(plane[0][:].bitcast(F32), 0.0)
         load_scales(0)
@@ -120,6 +137,16 @@ def tile_differentialselfattention_pa_kernel(
 
         nc.vector.memset(zero1[:], 0.0)
         nc.scalar.activation(out=junk1[:], in_=zero1[:], func=ACT.Sin)
+
+        idle_out = {}
+
+        def idle_matmuls(n):
+            if n and "t" not in idle_out:
+                idle_out["t"] = psum_m.tile([P, 1, 512], F32, name="idle_ps", tag="m")
+            for i in range(n):
+                nc.tensor.matmul(idle_out["t"][:, 0, :], lhsT=idle_in[:, 0:P], rhs=idle_in, start=True, stop=True)
+
+        idle_matmuls(WARM0)
 
         nc.vector.tensor_copy(out=tok[:], in_=tok_i[:])
         nc.vector.memset(freq[:, :, 0:1], 1.0)
@@ -231,7 +258,7 @@ def tile_differentialselfattention_pa_kernel(
                 nc.vector.quantize_mx(
                     out=xc[h][:, g, P * jj : P * (jj + 1)].bitcast(E5X4),
                     scales=xs[h][:, g, P * jj : P * (jj + 1)],
-                    in_=xg[j][:, g, :],
+                    in_=xg[j][:, g, :] if j < 4 else xg_late[:, g, jj, :],
                 )
 
         def xquant_late():
@@ -260,6 +287,7 @@ def tile_differentialselfattention_pa_kernel(
         load_words(1, 1)
         for j in range(4):
             xprep_transpose(j)
+            idle_matmuls(WARMJ)
             xprep_copy(j)
             xquant(j)
         bias_ps = psum_o.tile([P, P], F32, name="bias_ps", tag="o")
@@ -302,18 +330,48 @@ def tile_differentialselfattention_pa_kernel(
                 )
             live[("o", u)] = o
 
-        def mul(u):
+        def table_of(u):
             h = u // 32
-            js = slice(4 * h, 4 * h + 4)
+            return table[:, 4 * h : 4 * h + 4, :]
+
+        def mul(u):
             o = live.pop(("o", u))
-            xp = prod_pool.tile([P, 8, 2, 64], F32, name="xp", tag="xp")
+            if ("x", u // 2) not in live:
+                live[("x", u // 2)] = prod_pool.tile([P, 2, 8, 2, 64], F32, name="xp", tag="xp")
+            xp = live[("x", u // 2)]
             nc.vector.tensor_tensor(
-                out=xp[:],
+                out=xp[:, u % 2],
                 in0=o[:].to_broadcast([P, 8, 2, 64]),
-                in1=table[:, js, :].rearrange("p j (w h i) -> p (j w) h i", w=2, h=2),
+                in1=table_of(u).rearrange("p j (w h i) -> p (j w) h i", w=2, h=2),
                 op=ALU.mult,
             )
-            live[("x", u)] = xp
+
+        def second_half_copy(u):
+            sec = half_pool.tile([P, 4, 1, 64], F32, name="sec", tag="sec")
+            nc.scalar.copy(out=sec[:], in_=live[("o", u)][:, 1:8:2, :, :])
+            live[("sec", u)] = sec
+
+        def mul_first_half(u):
+            o = live.pop(("o", u))
+            xa = half_pool.tile([P, 4, 2, 64], F32, name="xa", tag="xa")
+            nc.vector.tensor_tensor(
+                out=xa[:],
+                in0=o[:, 0:8:2, :, :].to_broadcast([P, 4, 2, 64]),
+                in1=table_of(u).rearrange("p j (w h i) -> p j w h i", w=2, h=2)[:, :, 0, :, :],
+                op=ALU.mult,
+            )
+            live[("xa", u)] = xa
+
+        def mul_second_half(u):
+            sec = live.pop(("sec", u))
+            xb = half_pool.tile([P, 4, 2, 64], F32, name="xb", tag="xb")
+            nc.gpsimd.tensor_tensor(
+                out=xb[:],
+                in0=sec[:].to_broadcast([P, 4, 2, 64]),
+                in1=table_of(u).rearrange("p j (w h i) -> p j w h i", w=2, h=2)[:, :, 1, :, :],
+                op=ALU.mult,
+            )
+            live[("xb", u)] = xb
 
         def store(u, r):
             h, s = u // 32, u % 32
@@ -321,15 +379,40 @@ def tile_differentialselfattention_pa_kernel(
             head, part = sp // 2, sp % 2
             nc.sync.dma_start(
                 out=outs[2 * w + part][0, head].rearrange("(p j) d -> p j d", j=8)[:, 4 * h : 4 * h + 4, :],
-                in_=r[:],
+                in_=r,
             )
 
-        def add_store(u, on_vector):
-            xp = live.pop(("x", u))[:].rearrange("p (j w) h i -> p j w (h i)", w=2)
-            r = res_pool.tile([P, 4, P], F32, name="r", tag="r")
-            eng = nc.vector if on_vector else nc.gpsimd
-            eng.tensor_tensor(out=r[:], in0=xp[:, :, 0, :], in1=xp[:, :, 1, :], op=ALU.add)
-            store(u, r)
+        def add_halves_store(u):
+            xa = live.pop(("xa", u))
+            xb = live.pop(("xb", u))
+            r = res_pool.tile([P, 4, P], F32, name="rc", tag="rb")
+            nc.gpsimd.tensor_tensor(
+                out=r[:],
+                in0=xa[:].rearrange("p j h i -> p j (h i)"),
+                in1=xb[:].rearrange("p j h i -> p j (h i)"),
+                op=ALU.add,
+            )
+            store(u, r[:])
+
+        def add_store(us):
+            xp = live.pop(("x", us[0] // 2))[:].rearrange("p u (j w) h i -> p u j w (h i)", w=2)
+            r = res_pool.tile([P, 2, 4, P], F32, name="r", tag="r")
+            if len(us) == 1 or us[0] >= MERGE_TO:
+                for u in us:
+                    eng = nc.vector if u >= VADD_FROM else nc.gpsimd
+                    eng.tensor_tensor(
+                        out=r[:, u % 2], in0=xp[:, u % 2, :, 0, :], in1=xp[:, u % 2, :, 1, :], op=ALU.add
+                    )
+                    store(u, r[:, u % 2])
+            else:
+                nc.gpsimd.tensor_tensor(
+                    out=r[:].rearrange("p u j d -> p (u j) d"),
+                    in0=xp[:, :, :, 0, :].rearrange("p u j d -> p (u j) d"),
+                    in1=xp[:, :, :, 1, :].rearrange("p u j d -> p (u j) d"),
+                    op=ALU.add,
+                )
+                for u in us:
+                    store(u, r[:, u % 2])
 
         def zmul(u):
             h, s = u // 32, u % 32
@@ -360,9 +443,9 @@ def tile_differentialselfattention_pa_kernel(
 
         def copy_store(u):
             ob = live.pop(("ob", u))
-            r = res_pool.tile([P, 4, P], F32, name="r", tag="r")
+            r = res_pool.tile([P, 4, P], F32, name="rb", tag="rb")
             nc.scalar.copy(out=r[:], in_=ob[:])
-            store(u, r)
+            store(u, r[:])
 
         trig1 = trig_ops(1)
         fill1 = fill_ops(1, False)
@@ -383,42 +466,56 @@ def tile_differentialselfattention_pa_kernel(
                 for u in units(k):
                     mx(u)
             for u in units(k - 1):
-                if not is_b(u):
+                if kind(u) != "B":
                     tr(u)
             for u in units(k - 2):
-                if is_b(u):
+                if kind(u) == "B":
                     tradd(u)
-            if k == 3:
+            if k == TBK0:
                 tableb_transpose(0)
-            if k == 12:
+            if k == TBK1:
                 tableb_transpose(1)
-            if 8 <= k < 8 + 4:
-                xprep_transpose(k - 8 + 4)
+            if XK <= k < XK + 4:
+                xprep_transpose(k - XK + 4)
             if k <= 1:
                 for u in units(k):
                     mx(u)
             for u in units(k):
-                if not is_b(u):
+                if kind(u) != "B":
                     evac(u)
+            for u in units(k - 1):
+                if kind(u) == "C":
+                    second_half_copy(u)
             for u in units(k - 2):
-                if is_b(u):
+                if kind(u) == "B":
                     copy_store(u)
-            if k == 3:
+            if k == TBK0:
                 tableb_copy(0)
-            if k == 12:
+            if k == TBK1:
                 tableb_copy(1)
-            if 8 <= k < 8 + 4:
-                xprep_copy(k - 8 + 4)
+            if XK <= k < XK + 4:
+                xprep_copy(k - XK + 4)
             for op in scalar_extra.get(k, []):
                 op()
             for u in units(k - 0):
-                if is_b(u):
+                if kind(u) == "B":
                     zmul(u)
             for u in units(k - 1):
-                if not is_b(u):
+                if kind(u) == "A":
                     mul(u)
-            if k == 8 + 4:
-                xquant_late()
+                if kind(u) == "C":
+                    mul_first_half(u)
+            if WIDEQ:
+                if k == XK + 4:
+                    xquant_late()
+            elif XK + 1 <= k < XK + 5:
+                xquant(k - XK + 3)
             for u in units(k - 1):
-                if not is_b(u):
-                    add_store(u, u >= 62)
+                if kind(u) == "C":
+                    mul_second_half(u)
+            us = [u for u in units(k - 1) if kind(u) == "A"]
+            if us:
+                add_store(us)
+            for u in units(k - 1):
+                if kind(u) == "C":
+                    add_halves_store(u)

@@ -71,11 +71,9 @@ def tile_differentialselfattention_pa_kernel(
         xg_late = const.tile([P, 2, 4, 512], BF16, name="xg_late", align_bytes=64)
         xc = [const.tile([P, 2, 512], U32, name="xc%d" % h, align_bytes=64) for h in range(2)]
         xs = [const.tile([P, 2, 512], U8, name="xs%d" % h, align_bytes=64) for h in range(2)]
-        w_sb = [
-            [const.tile([P, 2, 2048], U8, name="w%d%d" % (w, c), align_bytes=64) for c in range(2)]
-            for w in range(2)
-        ]
-        plane = [const.tile([P, 2, 2048], U8, name="pl%d" % w, align_bytes=64) for w in range(2)]
+        runs = ((0, 0, 4), (0, 4, 12), (1, 0, 16))
+        w_sb = [const.tile([P, 2, 256 * n], U8, name="w%d_%d" % (w, s0), align_bytes=64) for (w, s0, n) in runs]
+        plane = [const.tile([P, 2, P * n], U8, name="pl%d_%d" % (w, s0), align_bytes=64) for (w, s0, n) in runs]
         ident = const.tile([P, P], F32, name="ident")
         perm = const.tile([P, P], F32, name="perm")
         bias_rows = const.tile([P, P], BF16, name="bias_rows")
@@ -98,28 +96,41 @@ def tile_differentialselfattention_pa_kernel(
         def load_x(j):
             nc.sync.dma_start(out=x_sb[j][:], in_=x_view[:, j, :])
 
-        def load_scales(w):
+        def load_scales(i):
+            w, s0, n = runs[i]
             for q in range(4):
                 nc.sync.dma_start(
-                    out=plane[w][32 * q : 32 * q + 4, :, :].bitcast(I32),
-                    in_=scales_in[w][:, 4 * q : 4 * q + 4, :].rearrange("g r n -> r g n").bitcast(I32),
+                    out=plane[i][32 * q : 32 * q + 4, :, :].bitcast(I32),
+                    in_=scales_in[w][:, 4 * q : 4 * q + 4, P * s0 : P * (s0 + n)].rearrange("g r n -> r g n").bitcast(I32),
                 )
 
-        def load_words(w, c):
+        def load_words(i):
+            w, s0, n = runs[i]
             nc.sync.dma_start(
-                out=w_sb[w][c][:].bitcast(I32),
-                in_=words_in[w][:, :, 2048 * c : 2048 * (c + 1)].rearrange("g p n -> p g n").bitcast(I32),
+                out=w_sb[i][:].bitcast(I32),
+                in_=words_in[w][:, :, 256 * s0 : 256 * (s0 + n)].rearrange("g p n -> p g n").bitcast(I32),
             )
 
-        for j in range(4):
-            load_x(j)
-        load_words(0, 0)
+        def run_of(w, sp):
+            for i in range(len(runs)):
+                if runs[i][0] == w and runs[i][1] <= sp < runs[i][1] + runs[i][2]:
+                    return i, sp - runs[i][1]
+            return None
+
+        nc.vector.memset(plane[0][:].bitcast(I32), 0)
+        load_x(0)
+        load_x(1)
+        load_scales(0)
+        load_x(2)
+        load_x(3)
+        load_words(0)
 
         if WARM0 or WARMJ:
             nc.vector.memset(idle_words[:], 0.0)
         nc.gpsimd.iota(tok_i[:].rearrange("p j o -> p (j o)"), pattern=[[1, 8]], base=0, channel_multiplier=8)
-        nc.gpsimd.memset(plane[0][:].bitcast(F32), 0.0)
-        load_scales(0)
+        nc.gpsimd.memset(plane[1][:].bitcast(F32), 0.0)
+        load_scales(1)
+        load_words(1)
         make_identity(nc, ident[:])
         nc.gpsimd.memset(bias_rows[32:64, :], 0.0)
         nc.gpsimd.memset(bias_rows[64:128, :], 0.0)
@@ -127,13 +138,12 @@ def tile_differentialselfattention_pa_kernel(
             nc.scalar.dma_start(
                 out=bias_rows[16 * w : 16 * w + 16, :], in_=bias_in[w].rearrange("(r c) -> r c", c=P)
             )
-        nc.gpsimd.memset(plane[1][:].bitcast(F32), 0.0)
+        nc.gpsimd.memset(plane[2][:].bitcast(F32), 0.0)
         nc.gpsimd.tensor_copy(out=perm[:, 0:64], in_=ident[:, 64:128])
         nc.gpsimd.tensor_copy(out=perm[:, 64:128], in_=ident[:, 0:64])
 
         for j in range(4, 8):
             load_x(j)
-        load_words(0, 1)
 
         nc.vector.memset(zero1[:], 0.0)
         nc.scalar.activation(out=junk1[:], in_=zero1[:], func=ACT.Sin)
@@ -282,9 +292,8 @@ def tile_differentialselfattention_pa_kernel(
         fill0 = fill_ops(0, True)
         for op in fill0[0:3]:
             op()
-        load_scales(1)
-        load_words(1, 0)
-        load_words(1, 1)
+        load_scales(2)
+        load_words(2)
         for j in range(4):
             xprep_transpose(j)
             idle_matmuls(WARMJ)
@@ -299,13 +308,13 @@ def tile_differentialselfattention_pa_kernel(
         def mx(u):
             h, s = u // 32, u % 32
             w, sp = s // 16, s % 16
-            c, sl = sp // 8, sp % 8
+            i, sl = run_of(w, sp)
             acc = psum_m.tile([P, 1, 512], F32, name="acc", tag="m")
             for g in range(2):
                 nc.tensor.matmul_mx(
                     out=acc[:, 0, :],
-                    lhsT=w_sb[w][c][:, g, 256 * sl : 256 * (sl + 1)].bitcast(E2X4),
-                    lhsT_scale=plane[w][:, g, P * sp : P * (sp + 1)],
+                    lhsT=w_sb[i][:, g, 256 * sl : 256 * (sl + 1)].bitcast(E2X4),
+                    lhsT_scale=plane[i][:, g, P * sl : P * (sl + 1)],
                     rhs=xc[h][:, g, :].bitcast(E5X4),
                     rhs_scale=xs[h][:, g, :],
                     start=(g == 0),

@@ -25,11 +25,17 @@ C2 = TWO_PI - C1
 WARM0 = 5
 WARMJ = 1
 XK = 8
-TBK0 = 3
+TBK0 = 4
 TBK1 = 12
 WIDEQ = True
 MERGE_TO = 0
 VADD_FROM = 62
+STARTUP = True
+GFILL = True
+BFIRST = False
+VFILL = True
+TAILSPLIT = False
+BIASFIRST = True
 
 
 def kind(u):
@@ -117,6 +123,11 @@ def tile_differentialselfattention_pa_kernel(
                     return i, sp - runs[i][1]
             return None
 
+        if BIASFIRST:
+            for w in range(2):
+                nc.scalar.dma_start(
+                    out=bias_rows[16 * w : 16 * w + 16, :], in_=bias_in[w].rearrange("(r c) -> r c", c=P)
+                )
         nc.vector.memset(plane[0][:].bitcast(I32), 0)
         load_x(0)
         load_x(1)
@@ -134,11 +145,12 @@ def tile_differentialselfattention_pa_kernel(
         make_identity(nc, ident[:])
         nc.gpsimd.memset(bias_rows[32:64, :], 0.0)
         nc.gpsimd.memset(bias_rows[64:128, :], 0.0)
-        for w in range(2):
-            nc.scalar.dma_start(
-                out=bias_rows[16 * w : 16 * w + 16, :], in_=bias_in[w].rearrange("(r c) -> r c", c=P)
-            )
-        nc.gpsimd.memset(plane[2][:].bitcast(F32), 0.0)
+        if not BIASFIRST:
+            for w in range(2):
+                nc.scalar.dma_start(
+                    out=bias_rows[16 * w : 16 * w + 16, :], in_=bias_in[w].rearrange("(r c) -> r c", c=P)
+                )
+
         nc.gpsimd.tensor_copy(out=perm[:, 0:64], in_=ident[:, 64:128])
         nc.gpsimd.tensor_copy(out=perm[:, 64:128], in_=ident[:, 0:64])
 
@@ -206,7 +218,11 @@ def tile_differentialselfattention_pa_kernel(
             ]
 
         def affine(on_gpsimd, out, in_, sign):
-            if on_gpsimd:
+            if on_gpsimd == "V":
+                nc.vector.tensor_scalar(
+                    out=out, in0=in_, scalar1=-sign, scalar2=sign, op0=ALU.mult, op1=ALU.add
+                )
+            elif on_gpsimd:
                 nc.gpsimd.tensor_scalar(
                     out=out, in0=in_, scalar1=-sign, scalar2=sign, op0=ALU.mult, op1=ALU.add
                 )
@@ -285,23 +301,44 @@ def tile_differentialselfattention_pa_kernel(
         )
         for op in trig_ops(0)[0:2]:
             op()
-        for q, s in ((q_c[0], sin_c[0]), (q_s[0], sin_s[0])):
-            nc.vector.scalar_tensor_tensor(
-                out=q[:, :, 0, :], in0=s[:], scalar=2.0, in1=s[:], op0=ALU.mult, op1=ALU.mult
-            )
+        def squares0():
+            for q, s in ((q_c[0], sin_c[0]), (q_s[0], sin_s[0])):
+                nc.vector.scalar_tensor_tensor(
+                    out=q[:, :, 0, :], in0=s[:], scalar=2.0, in1=s[:], op0=ALU.mult, op1=ALU.mult
+                )
+
         fill0 = fill_ops(0, True)
-        for op in fill0[0:3]:
-            op()
-        load_scales(2)
-        load_words(2)
+        if not VFILL:
+            squares0()
+            if BFIRST:
+                for op in fill_ops(0, "V")[3:6]:
+                    op()
+            for op in fill0[0:3]:
+                op()
+            if GFILL and not BFIRST:
+                for op in fill0[3:6]:
+                    op()
+
         for j in range(4):
             xprep_transpose(j)
             idle_matmuls(WARMJ)
             xprep_copy(j)
             xquant(j)
+        if VFILL:
+            squares0()
+            for op in fill_ops(0, "V")[0:3]:
+                op()
+            for op in fill0[3:6]:
+                op()
+            nc.vector.memset(plane[2][:].bitcast(I32), 0)
+            load_scales(2)
+            load_words(2)
         bias_ps = psum_o.tile([P, P], F32, name="bias_ps", tag="o")
         nc.tensor.transpose(bias_ps[:], bias_rows32[:], ident[:])
         nc.scalar.copy(out=bias_col[:], in_=bias_ps[:, 0:32])
+        if BFIRST:
+            tableb_transpose(0)
+            tableb_copy(0)
 
         live = {}
 
@@ -391,6 +428,15 @@ def tile_differentialselfattention_pa_kernel(
                 in_=r,
             )
 
+        def store_part(u, r, a):
+            h, s = u // 32, u % 32
+            w, sp = s // 16, s % 16
+            head, part = sp // 2, sp % 2
+            nc.sync.dma_start(
+                out=outs[2 * w + part][0, head].rearrange("(p j) d -> p j d", j=8)[:, 4 * h + 2 * a : 4 * h + 2 * a + 2, :],
+                in_=r,
+            )
+
         def add_halves_store(u):
             xa = live.pop(("xa", u))
             xb = live.pop(("xb", u))
@@ -409,10 +455,18 @@ def tile_differentialselfattention_pa_kernel(
             if len(us) == 1 or us[0] >= MERGE_TO:
                 for u in us:
                     eng = nc.vector if u >= VADD_FROM else nc.gpsimd
-                    eng.tensor_tensor(
-                        out=r[:, u % 2], in0=xp[:, u % 2, :, 0, :], in1=xp[:, u % 2, :, 1, :], op=ALU.add
-                    )
-                    store(u, r[:, u % 2])
+                    if TAILSPLIT and u == 63:
+                        for a in range(2):
+                            js = slice(2 * a, 2 * a + 2)
+                            eng.tensor_tensor(
+                                out=r[:, u % 2, js], in0=xp[:, u % 2, js, 0, :], in1=xp[:, u % 2, js, 1, :], op=ALU.add
+                            )
+                            store_part(u, r[:, u % 2, js], a)
+                    else:
+                        eng.tensor_tensor(
+                            out=r[:, u % 2], in0=xp[:, u % 2, :, 0, :], in1=xp[:, u % 2, :, 1, :], op=ALU.add
+                        )
+                        store(u, r[:, u % 2])
             else:
                 nc.gpsimd.tensor_tensor(
                     out=r[:].rearrange("p u j d -> p (u j) d"),
@@ -460,9 +514,9 @@ def tile_differentialselfattention_pa_kernel(
         fill1 = fill_ops(1, False)
         fill0_b = fill_ops(0, False)
         scalar_extra = {
-            0: fill0_b[3:4],
-            1: fill0_b[4:5],
-            2: fill0_b[5:6],
+            0: [] if GFILL else fill0_b[3:4],
+            1: [] if GFILL else fill0_b[4:5],
+            2: [] if GFILL else fill0_b[5:6],
             4: trig1[0:2],
             5: trig1[2:4],
             6: fill1[0:2],
@@ -471,25 +525,51 @@ def tile_differentialselfattention_pa_kernel(
         }
 
         for k in range(37):
-            if k > 1:
+            if BFIRST and k == 0:
+                mx(0)
+                mx(1)
+                mx(2)
+                mx(3)
+            elif BFIRST and k == 1:
+                tradd(0)
+                tr(2)
+            elif BFIRST and k == 2:
+                mx(4)
+                tradd(1)
+                tr(3)
+                mx(5)
+            elif STARTUP and k == 0:
+                mx(0)
+                mx(1)
+                mx(2)
+            elif STARTUP and k == 1:
+                tr(0)
+                mx(3)
+                tr(1)
+            elif STARTUP and k == 2:
+                mx(4)
+                tr(2)
+                mx(5)
+                tr(3)
+            if k > 1 and not (STARTUP and k == 2):
                 for u in units(k):
                     mx(u)
             for u in units(k - 1):
-                if kind(u) != "B":
+                if kind(u) != "B" and not (STARTUP and k <= 2):
                     tr(u)
             for u in units(k - 2):
-                if kind(u) == "B":
+                if kind(u) == "B" and not (BFIRST and u < 2):
                     tradd(u)
-            if k == TBK0:
+            if k == TBK0 and not BFIRST:
                 tableb_transpose(0)
             if k == TBK1:
                 tableb_transpose(1)
             if XK <= k < XK + 4:
                 xprep_transpose(k - XK + 4)
-            if k <= 1:
+            if k <= 1 and not STARTUP:
                 for u in units(k):
                     mx(u)
-            for u in units(k):
+            for u in units(k + 1) if (BFIRST and k == 0) else ([] if (BFIRST and k == 1) else units(k)):
                 if kind(u) != "B":
                     evac(u)
             for u in units(k - 1):
@@ -498,7 +578,7 @@ def tile_differentialselfattention_pa_kernel(
             for u in units(k - 2):
                 if kind(u) == "B":
                     copy_store(u)
-            if k == TBK0:
+            if k == TBK0 and not BFIRST:
                 tableb_copy(0)
             if k == TBK1:
                 tableb_copy(1)

@@ -33,6 +33,7 @@ VADD_FROM = 62
 STARTUP = True
 GFILL = True
 BFIRST = False
+LASTB = False
 VFILL = True
 TAILSPLIT = False
 BIASFIRST = True
@@ -43,6 +44,8 @@ def kind(u):
         return "B"
     if False:
         return "C"
+    if False:
+        return "D"
     return "A"
 
 
@@ -67,9 +70,10 @@ def tile_differentialselfattention_pa_kernel(
         prod_pool = ctx.enter_context(tc.tile_pool(name="prod", bufs=4))
         half_pool = ctx.enter_context(tc.tile_pool(name="half", bufs=2))
         z_pool = ctx.enter_context(tc.tile_pool(name="zp", bufs=2))
+        zh_pool = ctx.enter_context(tc.tile_pool(name="zh", bufs=2))
         res_pool = ctx.enter_context(tc.tile_pool(name="res", bufs=8))
-        psum_m = ctx.enter_context(tc.psum_pool(name="psm", bufs=4))
-        psum_o = ctx.enter_context(tc.psum_pool(name="pso", bufs=4))
+        psum_m = ctx.enter_context(tc.psum_pool(name="psm", bufs=3))
+        psum_o = ctx.enter_context(tc.psum_pool(name="pso", bufs=5))
         ctx.enter_context(tc.manual_schedule())
 
         x_sb = [const.tile([P, 1024], BF16, name="x%d" % j) for j in range(8)]
@@ -491,16 +495,51 @@ def tile_differentialselfattention_pa_kernel(
             )
             live[("z", u)] = z
 
+        def zmul_cos(u):
+            h, s = u // 32, u % 32
+            acc = live.pop(("acc", u))
+            zc = zh_pool.tile([P, 512], F32, name="zc", tag="zc")
+            nc.vector.scalar_tensor_tensor(
+                out=zc[:],
+                in0=acc[:, 0, :],
+                scalar=bias_col[:, s : s + 1],
+                in1=cs_b[h][:, 0, :],
+                op0=ALU.add,
+                op1=ALU.mult,
+            )
+            live[("zc", u)] = zc
+
+        def evac_keep(u):
+            s = u % 32
+            ut = ut_pool.tile([P, 512], F32, name="ut", tag="ut")
+            nc.scalar.activation(
+                out=ut[:], in_=live[("acc", u)][:, 0, :], func=ACT.Identity, bias=bias_col[:, s : s + 1], scale=1.0
+            )
+            live[("ut", u)] = ut
+
+        def zmul_sin(u):
+            h = u // 32
+            ut = live.pop(("ut", u))
+            zs = zh_pool.tile([P, 512], F32, name="zs", tag="zs")
+            nc.gpsimd.tensor_tensor(out=zs[:], in0=ut[:], in1=cs_b[h][:, 1, :], op=ALU.mult)
+            live[("zs", u)] = zs
+
         def tradd(u):
-            z = live.pop(("z", u))
+            if kind(u) == "D":
+                z0 = live.pop(("zc", u))[:]
+                z1 = live.pop(("zs", u))[:]
+            else:
+                z = live.pop(("z", u))
+                z0 = z[:, 0, :]
+                z1 = z[:, 1, :]
             ob = psum_o.tile([P, 4, P], F32, name="ob", tag="o")
             for jj in range(4):
                 cols = slice(P * jj, P * (jj + 1))
                 nc.tensor.matmul(
-                    ob[:, jj, :], lhsT=z[:, 0, cols], rhs=ident[:], start=True, stop=False, is_transpose=True
+                    ob[:, jj, :], lhsT=z0[:, cols], rhs=ident[:], start=True, stop=False, is_transpose=True
                 )
                 nc.tensor.matmul(
-                    ob[:, jj, :], lhsT=z[:, 1, cols], rhs=perm[:], start=False, stop=True, is_transpose=True
+                    ob[:, jj, :], lhsT=z1[:, cols], rhs=perm[:], start=False, stop=True, is_transpose=True
                 )
             live[("ob", u)] = ob
 
@@ -555,11 +594,13 @@ def tile_differentialselfattention_pa_kernel(
                 for u in units(k):
                     mx(u)
             for u in units(k - 1):
-                if kind(u) != "B" and not (STARTUP and k <= 2):
+                if kind(u) not in ("B", "D") and not (STARTUP and k <= 2):
                     tr(u)
             for u in units(k - 2):
-                if kind(u) == "B" and not (BFIRST and u < 2):
+                if kind(u) in ("B", "D") and not (BFIRST and u < 2) and not (LASTB and u == 63):
                     tradd(u)
+            if LASTB and k == 32:
+                tradd(63)
             if k == TBK0 and not BFIRST:
                 tableb_transpose(0)
             if k == TBK1:
@@ -570,14 +611,18 @@ def tile_differentialselfattention_pa_kernel(
                 for u in units(k):
                     mx(u)
             for u in units(k + 1) if (BFIRST and k == 0) else ([] if (BFIRST and k == 1) else units(k)):
-                if kind(u) != "B":
+                if kind(u) == "D":
+                    evac_keep(u)
+                elif kind(u) != "B":
                     evac(u)
             for u in units(k - 1):
                 if kind(u) == "C":
                     second_half_copy(u)
             for u in units(k - 2):
-                if kind(u) == "B":
+                if kind(u) in ("B", "D") and not (LASTB and u == 63):
                     copy_store(u)
+            if LASTB and k == 32:
+                copy_store(63)
             if k == TBK0 and not BFIRST:
                 tableb_copy(0)
             if k == TBK1:
@@ -589,6 +634,8 @@ def tile_differentialselfattention_pa_kernel(
             for u in units(k - 0):
                 if kind(u) == "B":
                     zmul(u)
+                if kind(u) == "D":
+                    zmul_cos(u)
             for u in units(k - 1):
                 if kind(u) == "A":
                     mul(u)
@@ -599,6 +646,9 @@ def tile_differentialselfattention_pa_kernel(
                     xquant_late()
             elif XK + 1 <= k < XK + 5:
                 xquant(k - XK + 3)
+            for u in units(k):
+                if kind(u) == "D":
+                    zmul_sin(u)
             for u in units(k - 1):
                 if kind(u) == "C":
                     mul_second_half(u)

@@ -33,6 +33,9 @@ VADD_FROM = 62
 STARTUP = True
 GFILL = True
 BFIRST = False
+THIN = True
+ZLATE = False
+XSORT = False
 LASTB = False
 VFILL = True
 TAILSPLIT = False
@@ -40,7 +43,7 @@ BIASFIRST = True
 
 
 def kind(u):
-    if u % 4 == 3 and 11 <= u < 63:
+    if (u % 4 == 3 and 11 <= u < 63) or u == 61:
         return "B"
     if False:
         return "C"
@@ -267,12 +270,22 @@ def tile_differentialselfattention_pa_kernel(
 
         xt_tiles = {}
 
+        x_sorted = [const.tile([P, 2, 2, P], F32, name="xsrt%d" % j) for j in range(4)]
+
+        def xprep_sort(j):
+            nc.scalar.copy(
+                out=x_sorted[j - 4][:], in_=x_sb[j][:].bitcast(F32).rearrange("p (g t u) -> p g u t", g=2, u=2)
+            )
+
         def xprep_transpose(j):
             xt = psum_o.tile([P, 4, P], F32, name="xt", tag="o")
             xw = x_sb[j][:].bitcast(F32)
             for g in range(2):
                 for u in range(2):
-                    nc.tensor.transpose(xt[:, 2 * g + u, :], xw[:, 256 * g + u : 256 * (g + 1) : 2], ident[:])
+                    if XSORT and j >= 4:
+                        nc.tensor.transpose(xt[:, 2 * g + u, :], x_sorted[j - 4][:, g, u, :], ident[:])
+                    else:
+                        nc.tensor.transpose(xt[:, 2 * g + u, :], xw[:, 256 * g + u : 256 * (g + 1) : 2], ident[:])
             xt_tiles[j] = xt
 
         def xprep_copy(j):
@@ -563,6 +576,20 @@ def tile_differentialselfattention_pa_kernel(
             8: fill1[4:6],
         }
 
+        if THIN:
+            scalar_extra = {
+                3: trig1[0:1],
+                4: trig1[1:2],
+                5: trig1[2:3],
+                6: trig1[3:4],
+                7: fill1[3:4],
+                8: fill1[4:5],
+                9: fill1[5:6],
+                13: fill1[0:1],
+                14: fill1[1:2],
+                15: fill1[2:3],
+            }
+
         for k in range(37):
             if BFIRST and k == 0:
                 mx(0)
@@ -629,18 +656,27 @@ def tile_differentialselfattention_pa_kernel(
                 tableb_copy(1)
             if XK <= k < XK + 4:
                 xprep_copy(k - XK + 4)
+            if XSORT and XK - 1 <= k < XK + 3:
+                xprep_sort(k - XK + 5)
             for op in scalar_extra.get(k, []):
                 op()
-            for u in units(k - 0):
-                if kind(u) == "B":
-                    zmul(u)
-                if kind(u) == "D":
-                    zmul_cos(u)
+            if not ZLATE:
+                for u in units(k - 0):
+                    if kind(u) == "B":
+                        zmul(u)
+                    if kind(u) == "D":
+                        zmul_cos(u)
             for u in units(k - 1):
                 if kind(u) == "A":
                     mul(u)
                 if kind(u) == "C":
                     mul_first_half(u)
+            if ZLATE:
+                for u in units(k - 0):
+                    if kind(u) == "B":
+                        zmul(u)
+                    if kind(u) == "D":
+                        zmul_cos(u)
             if WIDEQ:
                 if k == XK + 4:
                     xquant_late()

@@ -17,45 +17,53 @@ FLOPS = 2 * 1024 * 1024 * 4096
 
 P = 128
 TWO_PI = 6.283185307179586
-QUARTER_PI = 0.7853981633974483
-SQRT2 = 1.4142135623730951
+HALF_PI = 1.5707963267948966
 C1 = int(TWO_PI * 8192.0) / 8192.0
 C2 = TWO_PI - C1
 
 WARM0 = 5
-WARMJ = 1
-XK = 8
-TBK0 = 4
-TBK1 = 12
-WIDEQ = True
-MERGE_TO = 0
-VADD_FROM = 62
-STARTUP = True
-GFILL = True
-BFIRST = False
-THIN = True
-ZLATE = False
-XSORT = False
-LASTB = False
-VFILL = True
-TAILSPLIT = False
-BIASFIRST = True
+HEAD = "a0 A0 a1 a2 a3 g0 g1 g2 g3 x0 V0 x1 i1 V1 q0 A1 q1 A2 x2 S2 q2 A3 x3 S3 q3 b i2 B cV sS"
+B_FROM = 11
+B_TO = 63
+BMOD = 4
+BPH = 3
+FIRST_B = (0,)
+GROUP = 2
+LAGB = 2
+START = 'm1 m0 m2 t1 m3 t2 m4 t3 m5'
+SIDE = "3:g0 4:g1 5:g2 6:g3 6:x4 7:x5 8:x6 9:x7 10:b1 10:q"
+VADD_FROM = 63
 
 
 def kind(u):
-    if (u % 4 == 3 and 11 <= u < 63) or u == 61:
+    if u in FIRST_B or (u % BMOD == BPH and B_FROM <= u < B_TO) or u == 61:
         return "B"
-    if False:
-        return "C"
-    if False:
-        return "D"
     return "A"
 
 
-def units(k):
-    if 0 <= k < 32:
-        return [2 * k, 2 * k + 1]
-    return []
+def plan():
+    out = START.split()
+    u = max(int(x[1:]) for x in out if x[0] == "m") + 1
+    done = set(x for x in out)
+    prev = [v for v in range(u) if ("t%d" % v) not in done and kind(v) == "A"]
+    prevb = [[v for v in range(u) if ("a%d" % v) not in done and kind(v) == "B"]]
+    pend = list(SIDE.split())
+    k = 0
+    while u < 64 or prev or any(prevb):
+        new = list(range(u, min(64, u + GROUP)))
+        u += len(new)
+        out += ["m%d" % v for v in new]
+        out += ["t%d" % v for v in prev]
+        if len(prevb) >= LAGB or not new:
+            out += ["a%d" % v for v in prevb.pop(0)]
+        for item in pend:
+            at, tok = item.split(":")
+            if int(at) == k:
+                out.append(tok)
+        prev = [v for v in new if kind(v) == "A"]
+        prevb.append([v for v in new if kind(v) == "B"])
+        k += 1
+    return out
 
 
 def tile_differentialselfattention_pa_kernel(
@@ -70,11 +78,9 @@ def tile_differentialselfattention_pa_kernel(
     with ExitStack() as ctx:
         const = ctx.enter_context(tc.tile_pool(name="const", bufs=1))
         ut_pool = ctx.enter_context(tc.tile_pool(name="ut", bufs=4))
-        prod_pool = ctx.enter_context(tc.tile_pool(name="prod", bufs=4))
-        half_pool = ctx.enter_context(tc.tile_pool(name="half", bufs=2))
-        z_pool = ctx.enter_context(tc.tile_pool(name="zp", bufs=2))
-        zh_pool = ctx.enter_context(tc.tile_pool(name="zh", bufs=2))
-        res_pool = ctx.enter_context(tc.tile_pool(name="res", bufs=8))
+        prod_pool = ctx.enter_context(tc.tile_pool(name="prod", bufs=8))
+        z_pool = ctx.enter_context(tc.tile_pool(name="zp", bufs=3))
+        res_pool = ctx.enter_context(tc.tile_pool(name="res", bufs=10))
         psum_m = ctx.enter_context(tc.psum_pool(name="psm", bufs=3))
         psum_o = ctx.enter_context(tc.psum_pool(name="pso", bufs=5))
         ctx.enter_context(tc.manual_schedule())
@@ -95,10 +101,10 @@ def tile_differentialselfattention_pa_kernel(
         tok_i = const.tile([P, 8, 1], I32, name="tok_i")
         tok = const.tile([P, 8, 1], F32, name="tok")
         freq = const.tile([P, 1, 64], F32, name="freq")
-        table = const.tile([P, 8, 256], F32, name="table")
-        cc_a = [const.tile([P, 4, 2, 64], F32, name="cca%d" % h) for h in range(2)]
-        ss_a = [const.tile([P, 4, 2, 64], F32, name="ssa%d" % h) for h in range(2)]
+        table = [const.tile([P, 4, 2, 2, 64], F32, name="table%d" % h) for h in range(2)]
         cs_b = [const.tile([P, 2, 512], F32, name="csb%d" % h) for h in range(2)]
+        psi = [const.tile([P, 4, 64], F32, name="psi%d" % h) for h in range(2)]
+        abs_psi = [const.tile([P, 4, 1, 64], F32, name="absp%d" % h) for h in range(2)]
         zero1 = const.tile([P, 1], F32, name="zero1")
         junk1 = const.tile([P, 1], F32, name="junk1")
         idle_words = const.tile([P, 256], F32, name="idle_words")
@@ -130,11 +136,10 @@ def tile_differentialselfattention_pa_kernel(
                     return i, sp - runs[i][1]
             return None
 
-        if BIASFIRST:
-            for w in range(2):
-                nc.scalar.dma_start(
-                    out=bias_rows[16 * w : 16 * w + 16, :], in_=bias_in[w].rearrange("(r c) -> r c", c=P)
-                )
+        for w in range(2):
+            nc.scalar.dma_start(
+                out=bias_rows[16 * w : 16 * w + 16, :], in_=bias_in[w].rearrange("(r c) -> r c", c=P)
+            )
         nc.vector.memset(plane[0][:].bitcast(I32), 0)
         load_x(0)
         load_x(1)
@@ -142,30 +147,26 @@ def tile_differentialselfattention_pa_kernel(
         load_x(2)
         load_x(3)
         load_words(0)
-
-        if WARM0 or WARMJ:
-            nc.vector.memset(idle_words[:], 0.0)
-        nc.gpsimd.iota(tok_i[:].rearrange("p j o -> p (j o)"), pattern=[[1, 8]], base=0, channel_multiplier=8)
-        nc.gpsimd.memset(plane[1][:].bitcast(F32), 0.0)
-        load_scales(1)
-        load_words(1)
-        make_identity(nc, ident[:])
-        nc.gpsimd.memset(bias_rows[32:64, :], 0.0)
-        nc.gpsimd.memset(bias_rows[64:128, :], 0.0)
-        if not BIASFIRST:
-            for w in range(2):
-                nc.scalar.dma_start(
-                    out=bias_rows[16 * w : 16 * w + 16, :], in_=bias_in[w].rearrange("(r c) -> r c", c=P)
-                )
-
-        nc.gpsimd.tensor_copy(out=perm[:, 0:64], in_=ident[:, 64:128])
-        nc.gpsimd.tensor_copy(out=perm[:, 64:128], in_=ident[:, 0:64])
-
-        for j in range(4, 8):
-            load_x(j)
-
+        nc.vector.memset(idle_words[:], 0.0)
         nc.vector.memset(zero1[:], 0.0)
         nc.scalar.activation(out=junk1[:], in_=zero1[:], func=ACT.Sin)
+        nc.gpsimd.iota(tok_i[:].rearrange("p j o -> p (j o)"), pattern=[[1, 8]], base=0, channel_multiplier=8)
+        make_identity(nc, ident[:])
+        nc.gpsimd.memset(plane[1][:].bitcast(F32), 0.0)
+        nc.gpsimd.memset(bias_rows[32:64, :], 0.0)
+        nc.gpsimd.memset(bias_rows[64:128, :], 0.0)
+        for j in range(4, 8):
+            load_x(j)
+        load_scales(1)
+        load_words(1)
+        nc.gpsimd.memset(plane[2][:].bitcast(F32), 0.0)
+        load_scales(2)
+        load_words(2)
+        nc.gpsimd.tensor_scalar(
+            out=bias_rows32[:], in0=bias_rows[:], scalar1=1.0, scalar2=0.0, op0=ALU.mult, op1=ALU.add
+        )
+        nc.gpsimd.tensor_copy(out=perm[:, 0:64], in_=ident[:, 64:128])
+        nc.gpsimd.tensor_copy(out=perm[:, 64:128], in_=ident[:, 0:64])
 
         idle_out = {}
 
@@ -177,131 +178,96 @@ def tile_differentialselfattention_pa_kernel(
 
         idle_matmuls(WARM0)
 
-        nc.vector.tensor_copy(out=tok[:], in_=tok_i[:])
         nc.vector.memset(freq[:, :, 0:1], 1.0)
-        for m in range(6):
-            n = 2**m
-            nc.vector.tensor_scalar_mul(
-                out=freq[:, :, n : 2 * n], in0=freq[:, :, 0:n], scalar1=10000.0 ** (-n / 64.0)
-            )
+        nc.vector.tensor_copy(out=tok[:], in_=tok_i[:])
+        for n in (1, 4, 16):
+            for q in (1, 2, 3):
+                nc.vector.tensor_scalar_mul(
+                    out=freq[:, :, q * n : (q + 1) * n], in0=freq[:, :, 0:n], scalar1=10000.0 ** (-q * n / 64.0)
+                )
 
-        psi = [const.tile([P, 4, 64], F32, name="psi%d" % h) for h in range(2)]
-        sin_c = [const.tile([P, 4, 64], F32, name="sinc%d" % h) for h in range(2)]
-        sin_s = [const.tile([P, 4, 64], F32, name="sins%d" % h) for h in range(2)]
-        q_c = [const.tile([P, 4, 1, 64], F32, name="qc%d" % h) for h in range(2)]
-        q_s = [const.tile([P, 4, 1, 64], F32, name="qs%d" % h) for h in range(2)]
+        th = [const.tile([P, 4, 64], F32, name="th%d" % h) for h in range(2)]
+        ki = [const.tile([P, 4, 64], I32, name="ki%d" % h) for h in range(2)]
+        r1 = [const.tile([P, 4, 64], F32, name="r1%d" % h) for h in range(2)]
 
-        def table_angles(h):
+        def angle_ops(h):
             js = slice(4 * h, 4 * h + 4)
-            th = const.tile([P, 4, 64], F32, name="th%d" % h)
-            ki = const.tile([P, 4, 64], I32, name="ki%d" % h)
-            r1 = const.tile([P, 4, 64], F32, name="r1%d" % h)
-            nc.vector.tensor_tensor(
-                out=th[:],
-                in0=tok[:, js, :].to_broadcast([P, 4, 64]),
-                in1=freq[:].to_broadcast([P, 4, 64]),
-                op=ALU.mult,
-            )
-            nc.vector.tensor_scalar(
-                out=ki[:], in0=th[:], scalar1=1.0 / TWO_PI, scalar2=0.125, op0=ALU.mult, op1=ALU.add
-            )
-            nc.vector.scalar_tensor_tensor(out=r1[:], in0=ki[:], scalar=-C1, in1=th[:], op0=ALU.mult, op1=ALU.add)
-            nc.vector.scalar_tensor_tensor(
-                out=psi[h][:], in0=ki[:], scalar=-C2, in1=r1[:], op0=ALU.mult, op1=ALU.add
-            )
-
-        def trig_ops(h):
             return [
-                lambda: nc.scalar.activation(out=sin_c[h][:], in_=psi[h][:], func=ACT.Sin, scale=0.5),
-                lambda: nc.scalar.activation(
-                    out=sin_s[h][:], in_=psi[h][:], func=ACT.Sin, bias=-QUARTER_PI, scale=0.5
+                lambda: nc.vector.tensor_tensor(
+                    out=th[h][:],
+                    in0=tok[:, js, :].to_broadcast([P, 4, 64]),
+                    in1=freq[:].to_broadcast([P, 4, 64]),
+                    op=ALU.mult,
                 ),
-                lambda: nc.scalar.activation(
-                    out=q_c[h][:, :, 0, :], in_=sin_c[h][:], func=ACT.Square, scale=SQRT2
+                lambda: nc.vector.tensor_scalar(
+                    out=ki[h][:], in0=th[h][:], scalar1=1.0 / TWO_PI, scalar2=0.0, op0=ALU.mult, op1=ALU.add
                 ),
-                lambda: nc.scalar.activation(
-                    out=q_s[h][:, :, 0, :], in_=sin_s[h][:], func=ACT.Square, scale=SQRT2
+                lambda: nc.vector.scalar_tensor_tensor(
+                    out=r1[h][:], in0=ki[h][:], scalar=-C1, in1=th[h][:], op0=ALU.mult, op1=ALU.add
+                ),
+                lambda: nc.vector.scalar_tensor_tensor(
+                    out=psi[h][:], in0=ki[h][:], scalar=-C2, in1=r1[h][:], op0=ALU.mult, op1=ALU.add
                 ),
             ]
 
-        def affine(on_gpsimd, out, in_, sign):
-            if on_gpsimd == "V":
-                nc.vector.tensor_scalar(
-                    out=out, in0=in_, scalar1=-sign, scalar2=sign, op0=ALU.mult, op1=ALU.add
-                )
-            elif on_gpsimd:
-                nc.gpsimd.tensor_scalar(
-                    out=out, in0=in_, scalar1=-sign, scalar2=sign, op0=ALU.mult, op1=ALU.add
-                )
-            else:
-                nc.scalar.activation(out=out, in_=in_, func=ACT.Identity, bias=sign, scale=-sign)
-
-        def fill_ops(h, g):
-            js = slice(4 * h, 4 * h + 4)
+        def trig_ops(h):
+            t = table[h]
             return [
-                lambda: affine(
-                    g,
-                    table[:, js, :].rearrange("p j (k i) -> p j k i", i=64)[:, :, 0:4:3, :],
-                    q_c[h][:].to_broadcast([P, 4, 2, 64]),
-                    1.0,
+                lambda: nc.scalar.activation(out=abs_psi[h][:, :, 0, :], in_=psi[h][:], func=ACT.Abs),
+                lambda: nc.scalar.activation(out=t[:, :, 1, 0, :], in_=psi[h][:], func=ACT.Sin),
+                lambda: nc.scalar.activation(out=t[:, :, 1, 1, :], in_=psi[h][:], func=ACT.Sin, scale=-1.0),
+                lambda: nc.scalar.activation(
+                    out=t[:, :, 0, :, :],
+                    in_=abs_psi[h][:].to_broadcast([P, 4, 2, 64]),
+                    func=ACT.Sin,
+                    bias=HALF_PI,
+                    scale=-1.0,
                 ),
-                lambda: affine(g, table[:, js, 64:128], q_s[h][:, :, 0, :], 1.0),
-                lambda: affine(g, table[:, js, 128:192], q_s[h][:, :, 0, :], -1.0),
-                lambda: affine(g, cc_a[h][:], q_c[h][:].to_broadcast([P, 4, 2, 64]), 1.0),
-                lambda: affine(g, ss_a[h][:, :, 0, :], q_s[h][:, :, 0, :], 1.0),
-                lambda: affine(g, ss_a[h][:, :, 1, :], q_s[h][:, :, 0, :], -1.0),
             ]
 
         tb_ps = {}
 
         def tableb_transpose(h):
-            cps = psum_o.tile([P, 4, P], F32, name="cps", tag="o")
-            sps = psum_o.tile([P, 4, P], F32, name="sps", tag="o")
-            for jj in range(4):
-                nc.tensor.transpose(cps[:, jj, :], cc_a[h][:, jj, :, :].rearrange("p k i -> p (k i)"), ident[:])
-            for jj in range(4):
-                nc.tensor.transpose(sps[:, jj, :], ss_a[h][:, jj, :, :].rearrange("p k i -> p (k i)"), ident[:])
-            tb_ps[h] = (cps, sps)
+            for q in range(2):
+                ps = psum_o.tile([P, 4, P], F32, name="tbps", tag="o")
+                for jj in range(4):
+                    nc.tensor.transpose(
+                        ps[:, jj, :], table[h][:, jj, q, :, :].rearrange("p w i -> p (w i)"), ident[:]
+                    )
+                tb_ps[(h, q)] = ps
 
-        def tableb_copy(h):
-            cps, sps = tb_ps[h]
-            nc.scalar.copy(out=cs_b[h][:, 0, :], in_=cps[:].rearrange("p j t -> p (j t)"))
-            nc.scalar.copy(out=cs_b[h][:, 1, :], in_=sps[:].rearrange("p j t -> p (j t)"))
+        def tableb_copy(h, q, eng):
+            src = tb_ps[(h, q)][:].rearrange("p j t -> p (j t)")
+            if eng == "V":
+                nc.vector.tensor_copy(out=cs_b[h][:, q, :], in_=src)
+            else:
+                nc.scalar.copy(out=cs_b[h][:, q, :], in_=src)
 
         xt_tiles = {}
-
-        x_sorted = [const.tile([P, 2, 2, P], F32, name="xsrt%d" % j) for j in range(4)]
-
-        def xprep_sort(j):
-            nc.scalar.copy(
-                out=x_sorted[j - 4][:], in_=x_sb[j][:].bitcast(F32).rearrange("p (g t u) -> p g u t", g=2, u=2)
-            )
 
         def xprep_transpose(j):
             xt = psum_o.tile([P, 4, P], F32, name="xt", tag="o")
             xw = x_sb[j][:].bitcast(F32)
             for g in range(2):
                 for u in range(2):
-                    if XSORT and j >= 4:
-                        nc.tensor.transpose(xt[:, 2 * g + u, :], x_sorted[j - 4][:, g, u, :], ident[:])
-                    else:
-                        nc.tensor.transpose(xt[:, 2 * g + u, :], xw[:, 256 * g + u : 256 * (g + 1) : 2], ident[:])
+                    nc.tensor.transpose(xt[:, 2 * g + u, :], xw[:, 256 * g + u : 256 * (g + 1) : 2], ident[:])
             xt_tiles[j] = xt
 
-        def xprep_copy(j):
+        def xprep_copy(j, eng="S"):
             dst = xg[j][:] if j < 4 else xg_late[:, :, j - 4, :]
-            nc.scalar.copy(
-                out=dst.bitcast(F32).rearrange("p g (t u) -> p g t u", u=2),
-                in_=xt_tiles[j][:].rearrange("p (g u) t -> p g t u", u=2),
-            )
+            dst = dst.bitcast(F32).rearrange("p g (t u) -> p g t u", u=2)
+            src = xt_tiles[j][:].rearrange("p (g u) t -> p g t u", u=2)
+            if eng == "V":
+                nc.vector.tensor_copy(out=dst, in_=src)
+            else:
+                nc.scalar.copy(out=dst, in_=src)
 
         def xquant(j):
-            h, jj = j // 4, j % 4
             for g in range(2):
                 nc.vector.quantize_mx(
-                    out=xc[h][:, g, P * jj : P * (jj + 1)].bitcast(E5X4),
-                    scales=xs[h][:, g, P * jj : P * (jj + 1)],
-                    in_=xg[j][:, g, :] if j < 4 else xg_late[:, g, jj, :],
+                    out=xc[0][:, g, P * j : P * (j + 1)].bitcast(E5X4),
+                    scales=xs[0][:, g, P * j : P * (j + 1)],
+                    in_=xg[j][:, g, :],
                 )
 
         def xquant_late():
@@ -311,51 +277,40 @@ def tile_differentialselfattention_pa_kernel(
                 in_=xg_late[:].rearrange("p g j c -> p (g j c)"),
             )
 
-        table_angles(0)
-        table_angles(1)
-        nc.gpsimd.tensor_scalar(
-            out=bias_rows32[:], in0=bias_rows[:], scalar1=1.0, scalar2=0.0, op0=ALU.mult, op1=ALU.add
-        )
-        for op in trig_ops(0)[0:2]:
-            op()
-        def squares0():
-            for q, s in ((q_c[0], sin_c[0]), (q_s[0], sin_s[0])):
-                nc.vector.scalar_tensor_tensor(
-                    out=q[:, :, 0, :], in0=s[:], scalar=2.0, in1=s[:], op0=ALU.mult, op1=ALU.mult
-                )
+        a0, a1 = angle_ops(0), angle_ops(1)
+        tg0 = trig_ops(0)
 
-        fill0 = fill_ops(0, True)
-        if not VFILL:
-            squares0()
-            if BFIRST:
-                for op in fill_ops(0, "V")[3:6]:
-                    op()
-            for op in fill0[0:3]:
-                op()
-            if GFILL and not BFIRST:
-                for op in fill0[3:6]:
-                    op()
+        def head(token):
+            c, rest = token[0], token[1:]
+            if c == "a":
+                a0[int(rest)]()
+            elif c == "A":
+                a1[int(rest)]()
+            elif c == "g":
+                tg0[int(rest)]()
+            elif c == "x":
+                xprep_transpose(int(rest))
+            elif c == "i":
+                idle_matmuls(int(rest))
+            elif c == "S":
+                xprep_copy(int(rest), "S")
+            elif c == "V":
+                xprep_copy(int(rest), "V")
+            elif c == "q":
+                xquant(int(rest))
+            elif c == "b":
+                tableb_transpose(0)
+            elif c == "c":
+                tableb_copy(0, 0, rest)
+            elif c == "s":
+                tableb_copy(0, 1, rest)
+            elif c == "B":
+                ps = psum_o.tile([P, P], F32, name="bias_ps", tag="o")
+                nc.tensor.transpose(ps[:], bias_rows32[:], ident[:])
+                nc.scalar.copy(out=bias_col[:], in_=ps[:, 0:32])
 
-        for j in range(4):
-            xprep_transpose(j)
-            idle_matmuls(WARMJ)
-            xprep_copy(j)
-            xquant(j)
-        if VFILL:
-            squares0()
-            for op in fill_ops(0, "V")[0:3]:
-                op()
-            for op in fill0[3:6]:
-                op()
-            nc.vector.memset(plane[2][:].bitcast(I32), 0)
-            load_scales(2)
-            load_words(2)
-        bias_ps = psum_o.tile([P, P], F32, name="bias_ps", tag="o")
-        nc.tensor.transpose(bias_ps[:], bias_rows32[:], ident[:])
-        nc.scalar.copy(out=bias_col[:], in_=bias_ps[:, 0:32])
-        if BFIRST:
-            tableb_transpose(0)
-            tableb_copy(0)
+        for token in HEAD.split():
+            head(token)
 
         live = {}
 
@@ -386,55 +341,21 @@ def tile_differentialselfattention_pa_kernel(
 
         def tr(u):
             ut = live.pop(("ut", u))
-            o = psum_o.tile([P, 8, 1, 64], F32, name="o", tag="o")
+            o = psum_o.tile([P, 4, 1, P], F32, name="o", tag="o")
             for jj in range(4):
-                nc.tensor.transpose(
-                    o[:, 2 * jj : 2 * jj + 2, 0, :].rearrange("p m i -> p (m i)"), ut[:, P * jj : P * (jj + 1)], ident[:]
-                )
+                nc.tensor.transpose(o[:, jj, 0, :], ut[:, P * jj : P * (jj + 1)], ident[:])
             live[("o", u)] = o
-
-        def table_of(u):
-            h = u // 32
-            return table[:, 4 * h : 4 * h + 4, :]
 
         def mul(u):
             o = live.pop(("o", u))
-            if ("x", u // 2) not in live:
-                live[("x", u // 2)] = prod_pool.tile([P, 2, 8, 2, 64], F32, name="xp", tag="xp")
-            xp = live[("x", u // 2)]
+            xp = prod_pool.tile([P, 4, 2, 2, 64], F32, name="xp", tag="xp")
             nc.vector.tensor_tensor(
-                out=xp[:, u % 2],
-                in0=o[:].to_broadcast([P, 8, 2, 64]),
-                in1=table_of(u).rearrange("p j (w h i) -> p (j w) h i", w=2, h=2),
+                out=xp[:].rearrange("p j q w i -> p j q (w i)"),
+                in0=o[:].to_broadcast([P, 4, 2, P]),
+                in1=table[u // 32][:].rearrange("p j q w i -> p j q (w i)"),
                 op=ALU.mult,
             )
-
-        def second_half_copy(u):
-            sec = half_pool.tile([P, 4, 1, 64], F32, name="sec", tag="sec")
-            nc.scalar.copy(out=sec[:], in_=live[("o", u)][:, 1:8:2, :, :])
-            live[("sec", u)] = sec
-
-        def mul_first_half(u):
-            o = live.pop(("o", u))
-            xa = half_pool.tile([P, 4, 2, 64], F32, name="xa", tag="xa")
-            nc.vector.tensor_tensor(
-                out=xa[:],
-                in0=o[:, 0:8:2, :, :].to_broadcast([P, 4, 2, 64]),
-                in1=table_of(u).rearrange("p j (w h i) -> p j w h i", w=2, h=2)[:, :, 0, :, :],
-                op=ALU.mult,
-            )
-            live[("xa", u)] = xa
-
-        def mul_second_half(u):
-            sec = live.pop(("sec", u))
-            xb = half_pool.tile([P, 4, 2, 64], F32, name="xb", tag="xb")
-            nc.gpsimd.tensor_tensor(
-                out=xb[:],
-                in0=sec[:].to_broadcast([P, 4, 2, 64]),
-                in1=table_of(u).rearrange("p j (w h i) -> p j w h i", w=2, h=2)[:, :, 1, :, :],
-                op=ALU.mult,
-            )
-            live[("xb", u)] = xb
+            live[("x", u)] = xp
 
         def store(u, r):
             h, s = u // 32, u % 32
@@ -445,54 +366,12 @@ def tile_differentialselfattention_pa_kernel(
                 in_=r,
             )
 
-        def store_part(u, r, a):
-            h, s = u // 32, u % 32
-            w, sp = s // 16, s % 16
-            head, part = sp // 2, sp % 2
-            nc.sync.dma_start(
-                out=outs[2 * w + part][0, head].rearrange("(p j) d -> p j d", j=8)[:, 4 * h + 2 * a : 4 * h + 2 * a + 2, :],
-                in_=r,
-            )
-
-        def add_halves_store(u):
-            xa = live.pop(("xa", u))
-            xb = live.pop(("xb", u))
-            r = res_pool.tile([P, 4, P], F32, name="rc", tag="rb")
-            nc.gpsimd.tensor_tensor(
-                out=r[:],
-                in0=xa[:].rearrange("p j h i -> p j (h i)"),
-                in1=xb[:].rearrange("p j h i -> p j (h i)"),
-                op=ALU.add,
-            )
-            store(u, r[:])
-
-        def add_store(us):
-            xp = live.pop(("x", us[0] // 2))[:].rearrange("p u (j w) h i -> p u j w (h i)", w=2)
-            r = res_pool.tile([P, 2, 4, P], F32, name="r", tag="r")
-            if len(us) == 1 or us[0] >= MERGE_TO:
-                for u in us:
-                    eng = nc.vector if u >= VADD_FROM else nc.gpsimd
-                    if TAILSPLIT and u == 63:
-                        for a in range(2):
-                            js = slice(2 * a, 2 * a + 2)
-                            eng.tensor_tensor(
-                                out=r[:, u % 2, js], in0=xp[:, u % 2, js, 0, :], in1=xp[:, u % 2, js, 1, :], op=ALU.add
-                            )
-                            store_part(u, r[:, u % 2, js], a)
-                    else:
-                        eng.tensor_tensor(
-                            out=r[:, u % 2], in0=xp[:, u % 2, :, 0, :], in1=xp[:, u % 2, :, 1, :], op=ALU.add
-                        )
-                        store(u, r[:, u % 2])
-            else:
-                nc.gpsimd.tensor_tensor(
-                    out=r[:].rearrange("p u j d -> p (u j) d"),
-                    in0=xp[:, :, :, 0, :].rearrange("p u j d -> p (u j) d"),
-                    in1=xp[:, :, :, 1, :].rearrange("p u j d -> p (u j) d"),
-                    op=ALU.add,
-                )
-                for u in us:
-                    store(u, r[:, u % 2])
+        def add_store(u):
+            xp = live.pop(("x", u))
+            r = res_pool.tile([P, 4, 2, 64], F32, name="r", tag="r")
+            eng = nc.vector if u >= VADD_FROM else nc.gpsimd
+            eng.tensor_tensor(out=r[:], in0=xp[:, :, 0, :, :], in1=xp[:, :, 1, ::-1, :], op=ALU.add)
+            store(u, r[:].rearrange("p j w i -> p j (w i)"))
 
         def zmul(u):
             h, s = u // 32, u % 32
@@ -508,51 +387,16 @@ def tile_differentialselfattention_pa_kernel(
             )
             live[("z", u)] = z
 
-        def zmul_cos(u):
-            h, s = u // 32, u % 32
-            acc = live.pop(("acc", u))
-            zc = zh_pool.tile([P, 512], F32, name="zc", tag="zc")
-            nc.vector.scalar_tensor_tensor(
-                out=zc[:],
-                in0=acc[:, 0, :],
-                scalar=bias_col[:, s : s + 1],
-                in1=cs_b[h][:, 0, :],
-                op0=ALU.add,
-                op1=ALU.mult,
-            )
-            live[("zc", u)] = zc
-
-        def evac_keep(u):
-            s = u % 32
-            ut = ut_pool.tile([P, 512], F32, name="ut", tag="ut")
-            nc.scalar.activation(
-                out=ut[:], in_=live[("acc", u)][:, 0, :], func=ACT.Identity, bias=bias_col[:, s : s + 1], scale=1.0
-            )
-            live[("ut", u)] = ut
-
-        def zmul_sin(u):
-            h = u // 32
-            ut = live.pop(("ut", u))
-            zs = zh_pool.tile([P, 512], F32, name="zs", tag="zs")
-            nc.gpsimd.tensor_tensor(out=zs[:], in0=ut[:], in1=cs_b[h][:, 1, :], op=ALU.mult)
-            live[("zs", u)] = zs
-
         def tradd(u):
-            if kind(u) == "D":
-                z0 = live.pop(("zc", u))[:]
-                z1 = live.pop(("zs", u))[:]
-            else:
-                z = live.pop(("z", u))
-                z0 = z[:, 0, :]
-                z1 = z[:, 1, :]
+            z = live.pop(("z", u))
             ob = psum_o.tile([P, 4, P], F32, name="ob", tag="o")
             for jj in range(4):
                 cols = slice(P * jj, P * (jj + 1))
                 nc.tensor.matmul(
-                    ob[:, jj, :], lhsT=z0[:, cols], rhs=ident[:], start=True, stop=False, is_transpose=True
+                    ob[:, jj, :], lhsT=z[:, 0, cols], rhs=ident[:], start=True, stop=False, is_transpose=True
                 )
                 nc.tensor.matmul(
-                    ob[:, jj, :], lhsT=z1[:, cols], rhs=perm[:], start=False, stop=True, is_transpose=True
+                    ob[:, jj, :], lhsT=z[:, 1, cols], rhs=perm[:], start=False, stop=True, is_transpose=True
                 )
             live[("ob", u)] = ob
 
@@ -563,134 +407,33 @@ def tile_differentialselfattention_pa_kernel(
             store(u, r[:])
 
         trig1 = trig_ops(1)
-        fill1 = fill_ops(1, False)
-        fill0_b = fill_ops(0, False)
-        scalar_extra = {
-            0: [] if GFILL else fill0_b[3:4],
-            1: [] if GFILL else fill0_b[4:5],
-            2: [] if GFILL else fill0_b[5:6],
-            4: trig1[0:2],
-            5: trig1[2:4],
-            6: fill1[0:2],
-            7: fill1[2:4],
-            8: fill1[4:6],
-        }
 
-        if THIN:
-            scalar_extra = {
-                3: trig1[0:1],
-                4: trig1[1:2],
-                5: trig1[2:3],
-                6: trig1[3:4],
-                7: fill1[3:4],
-                8: fill1[4:5],
-                9: fill1[5:6],
-                13: fill1[0:1],
-                14: fill1[1:2],
-                15: fill1[2:3],
-            }
+        def do(token):
+            c, n = token[0], int(token[1:] or "0")
+            if c == "m":
+                mx(n)
+                if kind(n) == "B":
+                    zmul(n)
+                else:
+                    evac(n)
+            elif c == "t":
+                tr(n)
+                mul(n)
+                add_store(n)
+            elif c == "a":
+                tradd(n)
+                copy_store(n)
+            elif c == "x":
+                xprep_transpose(n)
+                xprep_copy(n)
+            elif c == "q":
+                xquant_late()
+            elif c == "b":
+                tableb_transpose(n)
+                tableb_copy(n, 0, "S")
+                tableb_copy(n, 1, "S")
+            elif c == "g":
+                trig1[n]()
 
-        for k in range(37):
-            if BFIRST and k == 0:
-                mx(0)
-                mx(1)
-                mx(2)
-                mx(3)
-            elif BFIRST and k == 1:
-                tradd(0)
-                tr(2)
-            elif BFIRST and k == 2:
-                mx(4)
-                tradd(1)
-                tr(3)
-                mx(5)
-            elif STARTUP and k == 0:
-                mx(0)
-                mx(1)
-                mx(2)
-            elif STARTUP and k == 1:
-                tr(0)
-                mx(3)
-                tr(1)
-            elif STARTUP and k == 2:
-                mx(4)
-                tr(2)
-                mx(5)
-                tr(3)
-            if k > 1 and not (STARTUP and k == 2):
-                for u in units(k):
-                    mx(u)
-            for u in units(k - 1):
-                if kind(u) not in ("B", "D") and not (STARTUP and k <= 2):
-                    tr(u)
-            for u in units(k - 2):
-                if kind(u) in ("B", "D") and not (BFIRST and u < 2) and not (LASTB and u == 63):
-                    tradd(u)
-            if LASTB and k == 32:
-                tradd(63)
-            if k == TBK0 and not BFIRST:
-                tableb_transpose(0)
-            if k == TBK1:
-                tableb_transpose(1)
-            if XK <= k < XK + 4:
-                xprep_transpose(k - XK + 4)
-            if k <= 1 and not STARTUP:
-                for u in units(k):
-                    mx(u)
-            for u in units(k + 1) if (BFIRST and k == 0) else ([] if (BFIRST and k == 1) else units(k)):
-                if kind(u) == "D":
-                    evac_keep(u)
-                elif kind(u) != "B":
-                    evac(u)
-            for u in units(k - 1):
-                if kind(u) == "C":
-                    second_half_copy(u)
-            for u in units(k - 2):
-                if kind(u) in ("B", "D") and not (LASTB and u == 63):
-                    copy_store(u)
-            if LASTB and k == 32:
-                copy_store(63)
-            if k == TBK0 and not BFIRST:
-                tableb_copy(0)
-            if k == TBK1:
-                tableb_copy(1)
-            if XK <= k < XK + 4:
-                xprep_copy(k - XK + 4)
-            if XSORT and XK - 1 <= k < XK + 3:
-                xprep_sort(k - XK + 5)
-            for op in scalar_extra.get(k, []):
-                op()
-            if not ZLATE:
-                for u in units(k - 0):
-                    if kind(u) == "B":
-                        zmul(u)
-                    if kind(u) == "D":
-                        zmul_cos(u)
-            for u in units(k - 1):
-                if kind(u) == "A":
-                    mul(u)
-                if kind(u) == "C":
-                    mul_first_half(u)
-            if ZLATE:
-                for u in units(k - 0):
-                    if kind(u) == "B":
-                        zmul(u)
-                    if kind(u) == "D":
-                        zmul_cos(u)
-            if WIDEQ:
-                if k == XK + 4:
-                    xquant_late()
-            elif XK + 1 <= k < XK + 5:
-                xquant(k - XK + 3)
-            for u in units(k):
-                if kind(u) == "D":
-                    zmul_sin(u)
-            for u in units(k - 1):
-                if kind(u) == "C":
-                    mul_second_half(u)
-            us = [u for u in units(k - 1) if kind(u) == "A"]
-            if us:
-                add_store(us)
-            for u in units(k - 1):
-                if kind(u) == "C":
-                    add_halves_store(u)
+        for token in plan():
+            do(token)

@@ -23,15 +23,17 @@ C2 = TWO_PI - C1
 
 WARM0 = 5
 HEAD = "a0 A0 a1 a2 a3 g0 g1 g2 g3 x0 V0 x1 i1 V1 q0 A1 q1 A2 x2 S2 q2 A3 x3 S3 q3 b i2 B cV sS"
-B_FROM = 11
+B_FROM = 7
 B_TO = 63
-BMOD = 4
-BPH = 3
+BMOD = 3
+BPH = 1
 FIRST_B = (0,)
-GROUP = 2
-LAGB = 2
+GROUP = 3
+XSORT = False
+PSM = 3
+LAGB = 1
 START = 'm1 m0 m2 t1 m3 t2 m4 t3 m5'
-SIDE = "3:g0 4:g1 5:g2 6:g3 6:x4 7:x5 8:x6 9:x7 10:b1 10:q"
+SIDE = "12:g0 14:g1 16:g2 18:g3 18:x4 20:x5 22:x6 24:x7 26:b1 26:q"
 VADD_FROM = 63
 
 
@@ -58,7 +60,7 @@ def plan():
             out += ["a%d" % v for v in prevb.pop(0)]
         for item in pend:
             at, tok = item.split(":")
-            if int(at) == k:
+            if u - len(new) <= int(at) < u:
                 out.append(tok)
         prev = [v for v in new if kind(v) == "A"]
         prevb.append([v for v in new if kind(v) == "B"])
@@ -81,8 +83,8 @@ def tile_differentialselfattention_pa_kernel(
         prod_pool = ctx.enter_context(tc.tile_pool(name="prod", bufs=8))
         z_pool = ctx.enter_context(tc.tile_pool(name="zp", bufs=3))
         res_pool = ctx.enter_context(tc.tile_pool(name="res", bufs=10))
-        psum_m = ctx.enter_context(tc.psum_pool(name="psm", bufs=3))
-        psum_o = ctx.enter_context(tc.psum_pool(name="pso", bufs=5))
+        psum_m = ctx.enter_context(tc.psum_pool(name="psm", bufs=PSM))
+        psum_o = ctx.enter_context(tc.psum_pool(name="pso", bufs=8 - PSM))
         ctx.enter_context(tc.manual_schedule())
 
         x_sb = [const.tile([P, 1024], BF16, name="x%d" % j) for j in range(8)]
@@ -244,13 +246,20 @@ def tile_differentialselfattention_pa_kernel(
                 nc.scalar.copy(out=cs_b[h][:, q, :], in_=src)
 
         xt_tiles = {}
+        x_sorted = [const.tile([P, 2, 2, P], F32, name="xsrt%d" % j) for j in range(4)]
+
+        def xprep_sort(j):
+            nc.scalar.copy(
+                out=x_sorted[j - 4][:], in_=x_sb[j][:].bitcast(F32).rearrange("p (g t u) -> p g u t", g=2, u=2)
+            )
 
         def xprep_transpose(j):
             xt = psum_o.tile([P, 4, P], F32, name="xt", tag="o")
             xw = x_sb[j][:].bitcast(F32)
             for g in range(2):
                 for u in range(2):
-                    nc.tensor.transpose(xt[:, 2 * g + u, :], xw[:, 256 * g + u : 256 * (g + 1) : 2], ident[:])
+                    src = x_sorted[j - 4][:, g, u, :] if (XSORT and j >= 4) else xw[:, 256 * g + u : 256 * (g + 1) : 2]
+                    nc.tensor.transpose(xt[:, 2 * g + u, :], src, ident[:])
             xt_tiles[j] = xt
 
         def xprep_copy(j, eng="S"):
@@ -426,6 +435,8 @@ def tile_differentialselfattention_pa_kernel(
             elif c == "x":
                 xprep_transpose(n)
                 xprep_copy(n)
+            elif c == "s":
+                xprep_sort(n)
             elif c == "q":
                 xquant_late()
             elif c == "b":

@@ -29,17 +29,32 @@ BMOD = 3
 BPH = 1
 FIRST_B = (0,)
 GROUP = 3
+DMOD = 64
+DPH = ()
+D_FROM = 10
+D_TO = 58
+LAGD = 2
+E_SET = (12, 30, 48)
+TAIL = 2
+BSTORE = True
+VSTORE = True
+LASTB = (61,)
+UTB = 4
 XSORT = False
 PSM = 3
 LAGB = 1
-START = 'm1 m0 m2 t1 m3 t2 m4 t3 m5'
+START = 'm1 m0 m2 t1 m3 m4 t2 t3 m5'
 SIDE = "12:g0 14:g1 16:g2 18:g3 18:x4 20:x5 22:x6 24:x7 26:b1 26:q"
 VADD_FROM = 63
 
 
 def kind(u):
-    if u in FIRST_B or (u % BMOD == BPH and B_FROM <= u < B_TO) or u == 61:
+    if u in FIRST_B or (u % BMOD == BPH and B_FROM <= u < B_TO) or u in LASTB:
         return "B"
+    if u % DMOD in DPH and D_FROM <= u < D_TO:
+        return "D"
+    if u in E_SET:
+        return "E"
     return "A"
 
 
@@ -47,23 +62,27 @@ def plan():
     out = START.split()
     u = max(int(x[1:]) for x in out if x[0] == "m") + 1
     done = set(x for x in out)
-    prev = [v for v in range(u) if ("t%d" % v) not in done and kind(v) == "A"]
+    prev = [v for v in range(u) if ("t%d" % v) not in done and kind(v) in ("A", "E")]
     prevb = [[v for v in range(u) if ("a%d" % v) not in done and kind(v) == "B"]]
+    prevd = [[]]
     pend = list(SIDE.split())
     k = 0
-    while u < 64 or prev or any(prevb):
+    while u < 64 or prev or any(prevb) or any(prevd):
         new = list(range(u, min(64, u + GROUP)))
         u += len(new)
         out += ["m%d" % v for v in new]
         out += ["t%d" % v for v in prev]
         if len(prevb) >= LAGB or not new:
             out += ["a%d" % v for v in prevb.pop(0)]
+        if len(prevd) >= LAGD or not new:
+            out += ["a%d" % v for v in prevd.pop(0)]
         for item in pend:
             at, tok = item.split(":")
             if u - len(new) <= int(at) < u:
                 out.append(tok)
-        prev = [v for v in new if kind(v) == "A"]
+        prev = [v for v in new if kind(v) in ("A", "E")]
         prevb.append([v for v in new if kind(v) == "B"])
+        prevd.append([v for v in new if kind(v) == "D"])
         k += 1
     return out
 
@@ -79,9 +98,11 @@ def tile_differentialselfattention_pa_kernel(
 
     with ExitStack() as ctx:
         const = ctx.enter_context(tc.tile_pool(name="const", bufs=1))
-        ut_pool = ctx.enter_context(tc.tile_pool(name="ut", bufs=4))
+        ut_pool = ctx.enter_context(tc.tile_pool(name="ut", bufs=UTB))
         prod_pool = ctx.enter_context(tc.tile_pool(name="prod", bufs=8))
         z_pool = ctx.enter_context(tc.tile_pool(name="zp", bufs=3))
+        zh_pool = ctx.enter_context(tc.tile_pool(name="zh", bufs=4))
+        oc_pool = ctx.enter_context(tc.tile_pool(name="oc", bufs=2))
         res_pool = ctx.enter_context(tc.tile_pool(name="res", bufs=10))
         psum_m = ctx.enter_context(tc.psum_pool(name="psm", bufs=PSM))
         psum_o = ctx.enter_context(tc.psum_pool(name="pso", bufs=8 - PSM))
@@ -366,11 +387,33 @@ def tile_differentialselfattention_pa_kernel(
             )
             live[("x", u)] = xp
 
+        def mul_gpsimd(u):
+            o = live.pop(("o", u))
+            oc = oc_pool.tile([P, 4, 1, P], F32, name="oc", tag="oc")
+            nc.scalar.copy(out=oc[:], in_=o[:])
+            xp = prod_pool.tile([P, 4, 2, 2, 64], F32, name="xp", tag="xp")
+            nc.gpsimd.tensor_tensor(
+                out=xp[:].rearrange("p j q w i -> p j q (w i)"),
+                in0=oc[:].to_broadcast([P, 4, 2, P]),
+                in1=table[u // 32][:].rearrange("p j q w i -> p j q (w i)"),
+                op=ALU.mult,
+            )
+            live[("x", u)] = xp
+
+        def store_part(u, r, a, n):
+            h, s = u // 32, u % 32
+            w, sp = s // 16, s % 16
+            head, part = sp // 2, sp % 2
+            (nc.scalar if VSTORE and u >= VADD_FROM else nc.sync).dma_start(
+                out=outs[2 * w + part][0, head].rearrange("(p j) d -> p j d", j=8)[:, 4 * h + a : 4 * h + a + n, :],
+                in_=r,
+            )
+
         def store(u, r):
             h, s = u // 32, u % 32
             w, sp = s // 16, s % 16
             head, part = sp // 2, sp % 2
-            nc.sync.dma_start(
+            (nc.scalar if BSTORE else nc.sync).dma_start(
                 out=outs[2 * w + part][0, head].rearrange("(p j) d -> p j d", j=8)[:, 4 * h : 4 * h + 4, :],
                 in_=r,
             )
@@ -379,8 +422,11 @@ def tile_differentialselfattention_pa_kernel(
             xp = live.pop(("x", u))
             r = res_pool.tile([P, 4, 2, 64], F32, name="r", tag="r")
             eng = nc.vector if u >= VADD_FROM else nc.gpsimd
-            eng.tensor_tensor(out=r[:], in0=xp[:, :, 0, :, :], in1=xp[:, :, 1, ::-1, :], op=ALU.add)
-            store(u, r[:].rearrange("p j w i -> p j (w i)"))
+            n = 4 // (TAIL if u == 63 else 1)
+            for a in range(0, 4, n):
+                js = slice(a, a + n)
+                eng.tensor_tensor(out=r[:, js], in0=xp[:, js, 0, :, :], in1=xp[:, js, 1, ::-1, :], op=ALU.add)
+                store_part(u, r[:, js].rearrange("p j w i -> p j (w i)"), a, n)
 
         def zmul(u):
             h, s = u // 32, u % 32
@@ -396,16 +442,51 @@ def tile_differentialselfattention_pa_kernel(
             )
             live[("z", u)] = z
 
+        def zmul_cos(u):
+            h, s = u // 32, u % 32
+            acc = live.pop(("acc", u))
+            zc = zh_pool.tile([P, 512], F32, name="zc", tag="zc")
+            nc.vector.scalar_tensor_tensor(
+                out=zc[:],
+                in0=acc[:, 0, :],
+                scalar=bias_col[:, s : s + 1],
+                in1=cs_b[h][:, 0, :],
+                op0=ALU.add,
+                op1=ALU.mult,
+            )
+            live[("zc", u)] = zc
+
+        def evac_keep(u):
+            s = u % 32
+            ut = ut_pool.tile([P, 512], F32, name="ut", tag="ut")
+            nc.scalar.activation(
+                out=ut[:], in_=live[("acc", u)][:, 0, :], func=ACT.Identity, bias=bias_col[:, s : s + 1], scale=1.0
+            )
+            live[("ut", u)] = ut
+
+        def zmul_sin(u):
+            h = u // 32
+            ut = live.pop(("ut", u))
+            zs = zh_pool.tile([P, 512], F32, name="zs", tag="zs")
+            nc.gpsimd.tensor_tensor(out=zs[:], in0=ut[:], in1=cs_b[h][:, 1, :], op=ALU.mult)
+            live[("zs", u)] = zs
+
         def tradd(u):
-            z = live.pop(("z", u))
+            if kind(u) == "D":
+                z0 = live.pop(("zc", u))[:]
+                z1 = live.pop(("zs", u))[:]
+            else:
+                z = live.pop(("z", u))
+                z0 = z[:, 0, :]
+                z1 = z[:, 1, :]
             ob = psum_o.tile([P, 4, P], F32, name="ob", tag="o")
             for jj in range(4):
                 cols = slice(P * jj, P * (jj + 1))
                 nc.tensor.matmul(
-                    ob[:, jj, :], lhsT=z[:, 0, cols], rhs=ident[:], start=True, stop=False, is_transpose=True
+                    ob[:, jj, :], lhsT=z0[:, cols], rhs=ident[:], start=True, stop=False, is_transpose=True
                 )
                 nc.tensor.matmul(
-                    ob[:, jj, :], lhsT=z[:, 1, cols], rhs=perm[:], start=False, stop=True, is_transpose=True
+                    ob[:, jj, :], lhsT=z1[:, cols], rhs=perm[:], start=False, stop=True, is_transpose=True
                 )
             live[("ob", u)] = ob
 
@@ -423,11 +504,18 @@ def tile_differentialselfattention_pa_kernel(
                 mx(n)
                 if kind(n) == "B":
                     zmul(n)
+                elif kind(n) == "D":
+                    evac_keep(n)
+                    zmul_cos(n)
+                    zmul_sin(n)
                 else:
                     evac(n)
             elif c == "t":
                 tr(n)
-                mul(n)
+                if kind(n) == "E":
+                    mul_gpsimd(n)
+                else:
+                    mul(n)
                 add_store(n)
             elif c == "a":
                 tradd(n)

@@ -23,10 +23,14 @@ C2 = TWO_PI - C1
 
 WARM0 = 5
 HEAD = "a0 A0 a1 a2 a3 g0 g1 g2 g3 x0 V0 x1 i1 V1 q0 A1 q1 A2 x2 S2 q2 A3 x3 S3 q3 b i2 B cV sS"
-B_FROM = 7
+B_FROM = 99
 B_TO = 63
-BMOD = 3
-BPH = 1
+BMOD = 4
+BPH = 3
+BQ = 64
+BZ = 63
+B_SET = (7, 10, 13, 16, 19, 22, 25, 28, 31, 34, 37, 40, 43, 46, 49, 52, 55, 58, 61)
+PRB = 8
 FIRST_B = (0,)
 GROUP = 3
 DMOD = 64
@@ -36,20 +40,26 @@ D_TO = 58
 LAGD = 2
 E_SET = (12, 30, 48)
 TAIL = 2
+MERGE = False
+M_FROM = 6
+M_TO = 60
+PAIRB = 4
+RESB = 8
 BSTORE = True
+HALVES = ()
 VSTORE = True
 LASTB = (61,)
 UTB = 4
-XSORT = False
+XSORT = True
 PSM = 3
 LAGB = 1
 START = 'm1 m0 m2 t1 m3 m4 t2 t3 m5'
-SIDE = "12:g0 14:g1 16:g2 18:g3 18:x4 20:x5 22:x6 24:x7 26:b1 26:q"
+SIDE = '15:g0 18:g1 21:g2 24:g3 9:s4 12:s5 12:x4 15:s6 15:x5 18:s7 18:x6 21:x7 24:q 27:b1'
 VADD_FROM = 63
 
 
 def kind(u):
-    if u in FIRST_B or (u % BMOD == BPH and B_FROM <= u < B_TO) or u in LASTB:
+    if u in B_SET or u in FIRST_B or (u % BMOD == BPH and B_FROM <= u < B_TO and (u // 3) % BQ != BZ) or u in LASTB:
         return "B"
     if u % DMOD in DPH and D_FROM <= u < D_TO:
         return "D"
@@ -87,6 +97,26 @@ def plan():
     return out
 
 
+def pairs():
+    out = {}
+    if MERGE:
+        todo = []
+        for token in plan():
+            if token[0] == "m":
+                todo = []
+            if token[0] == "t":
+                n = int(token[1:])
+                if kind(n) == "A" and M_FROM <= n < M_TO:
+                    todo.append(n)
+                    if len(todo) == 2:
+                        out[todo[0]], out[todo[1]] = todo[1], todo[0]
+                        todo = []
+    return out
+
+
+PAIRED = pairs()
+
+
 def tile_differentialselfattention_pa_kernel(
     tc, x, Wq_words, Wq_scales, bq, Wk_words, Wk_scales, bk, out_0, out_1, out_2, out_3
 ):
@@ -99,16 +129,21 @@ def tile_differentialselfattention_pa_kernel(
     with ExitStack() as ctx:
         const = ctx.enter_context(tc.tile_pool(name="const", bufs=1))
         ut_pool = ctx.enter_context(tc.tile_pool(name="ut", bufs=UTB))
-        prod_pool = ctx.enter_context(tc.tile_pool(name="prod", bufs=8))
+        prod_pool = ctx.enter_context(tc.tile_pool(name="prod", bufs=PRB))
+        pair_pool = ctx.enter_context(tc.tile_pool(name="pair", bufs=PAIRB))
         z_pool = ctx.enter_context(tc.tile_pool(name="zp", bufs=3))
         zh_pool = ctx.enter_context(tc.tile_pool(name="zh", bufs=4))
         oc_pool = ctx.enter_context(tc.tile_pool(name="oc", bufs=2))
-        res_pool = ctx.enter_context(tc.tile_pool(name="res", bufs=10))
+        res_pool = ctx.enter_context(tc.tile_pool(name="res", bufs=RESB))
         psum_m = ctx.enter_context(tc.psum_pool(name="psm", bufs=PSM))
         psum_o = ctx.enter_context(tc.psum_pool(name="pso", bufs=8 - PSM))
         ctx.enter_context(tc.manual_schedule())
 
         x_sb = [const.tile([P, 1024], BF16, name="x%d" % j) for j in range(8)]
+        x_half = {}
+        for j in HALVES:
+            for g in range(2):
+                x_half[(j, g)] = const.tile([P, 512], BF16, name="xh%d_%d" % (j, g))
         xg = [const.tile([P, 2, 512], BF16, name="xg%d" % j, align_bytes=64) for j in range(4)]
         xg_late = const.tile([P, 2, 4, 512], BF16, name="xg_late", align_bytes=64)
         xc = [const.tile([P, 2, 512], U32, name="xc%d" % h, align_bytes=64) for h in range(2)]
@@ -136,7 +171,11 @@ def tile_differentialselfattention_pa_kernel(
         x_view = x[0].rearrange("(p j) k -> p j k", j=8)
 
         def load_x(j):
-            nc.sync.dma_start(out=x_sb[j][:], in_=x_view[:, j, :])
+            if j in HALVES:
+                for g in range(2):
+                    nc.sync.dma_start(out=x_half[(j, g)][:], in_=x_view[:, j, 512 * g : 512 * (g + 1)])
+            else:
+                nc.sync.dma_start(out=x_sb[j][:], in_=x_view[:, j, :])
 
         def load_scales(i):
             w, s0, n = runs[i]
@@ -283,6 +322,28 @@ def tile_differentialselfattention_pa_kernel(
                     nc.tensor.transpose(xt[:, 2 * g + u, :], src, ident[:])
             xt_tiles[j] = xt
 
+        def half_transpose(j, g):
+            xt = psum_o.tile([P, 2, P], F32, name="xth", tag="o")
+            xw = (x_half[(j, g)][:] if j in HALVES else x_sb[j][:, 512 * g : 512 * (g + 1)]).bitcast(F32)
+            for u in range(2):
+                nc.tensor.transpose(xt[:, u, :], xw[:, u:256:2], ident[:])
+            xt_tiles[(j, g)] = xt
+
+        def half_copy(j, g, eng):
+            dst = xg[j][:, g, :].bitcast(F32).rearrange("p (t u) -> p t u", u=2)
+            src = xt_tiles[(j, g)][:].rearrange("p u t -> p t u")
+            if eng == "V":
+                nc.vector.tensor_copy(out=dst, in_=src)
+            else:
+                nc.scalar.copy(out=dst, in_=src)
+
+        def half_quant(j, g):
+            nc.vector.quantize_mx(
+                out=xc[0][:, g, P * j : P * (j + 1)].bitcast(E5X4),
+                scales=xs[0][:, g, P * j : P * (j + 1)],
+                in_=xg[j][:, g, :],
+            )
+
         def xprep_copy(j, eng="S"):
             dst = xg[j][:] if j < 4 else xg_late[:, :, j - 4, :]
             dst = dst.bitcast(F32).rearrange("p g (t u) -> p g t u", u=2)
@@ -312,6 +373,15 @@ def tile_differentialselfattention_pa_kernel(
 
         def head(token):
             c, rest = token[0], token[1:]
+            if rest[0:1] in ("l", "h"):
+                j, g = int(rest[1:]), 0 if rest[0] == "l" else 1
+                if c == "x":
+                    half_transpose(j, g)
+                elif c == "q":
+                    half_quant(j, g)
+                else:
+                    half_copy(j, g, c)
+                return
             if c == "a":
                 a0[int(rest)]()
             elif c == "A":
@@ -378,14 +448,21 @@ def tile_differentialselfattention_pa_kernel(
 
         def mul(u):
             o = live.pop(("o", u))
-            xp = prod_pool.tile([P, 4, 2, 2, 64], F32, name="xp", tag="xp")
+            if u in PAIRED:
+                first = min(u, PAIRED[u])
+                if ("xx", first) not in live:
+                    live[("xx", first)] = pair_pool.tile([P, 8, 2, 2, 64], F32, name="xx", tag="xx")
+                xp = live[("xx", first)][:, 0:4] if u == first else live[("xx", first)][:, 4:8]
+            else:
+                xp = prod_pool.tile([P, 4, 2, 2, 64], F32, name="xp", tag="xp")[:]
             nc.vector.tensor_tensor(
-                out=xp[:].rearrange("p j q w i -> p j q (w i)"),
+                out=xp.rearrange("p j q w i -> p j q (w i)"),
                 in0=o[:].to_broadcast([P, 4, 2, P]),
                 in1=table[u // 32][:].rearrange("p j q w i -> p j q (w i)"),
                 op=ALU.mult,
             )
-            live[("x", u)] = xp
+            if u not in PAIRED:
+                live[("x", u)] = xp
 
         def mul_gpsimd(u):
             o = live.pop(("o", u))
@@ -398,7 +475,7 @@ def tile_differentialselfattention_pa_kernel(
                 in1=table[u // 32][:].rearrange("p j q w i -> p j q (w i)"),
                 op=ALU.mult,
             )
-            live[("x", u)] = xp
+            live[("x", u)] = xp[:]
 
         def store_part(u, r, a, n):
             h, s = u // 32, u % 32
@@ -427,6 +504,13 @@ def tile_differentialselfattention_pa_kernel(
                 js = slice(a, a + n)
                 eng.tensor_tensor(out=r[:, js], in0=xp[:, js, 0, :, :], in1=xp[:, js, 1, ::-1, :], op=ALU.add)
                 store_part(u, r[:, js].rearrange("p j w i -> p j (w i)"), a, n)
+
+        def add_store_pair(u, v):
+            xx = live.pop(("xx", u))
+            r = res_pool.tile([P, 8, 2, 64], F32, name="rr", tag="rr")
+            nc.gpsimd.tensor_tensor(out=r[:], in0=xx[:, :, 0, :, :], in1=xx[:, :, 1, ::-1, :], op=ALU.add)
+            store_part(u, r[:, 0:4].rearrange("p j w i -> p j (w i)"), 0, 4)
+            store_part(v, r[:, 4:8].rearrange("p j w i -> p j (w i)"), 0, 4)
 
         def zmul(u):
             h, s = u // 32, u % 32
@@ -516,7 +600,10 @@ def tile_differentialselfattention_pa_kernel(
                     mul_gpsimd(n)
                 else:
                     mul(n)
-                add_store(n)
+                if n not in PAIRED:
+                    add_store(n)
+                elif PAIRED[n] < n:
+                    add_store_pair(PAIRED[n], n)
             elif c == "a":
                 tradd(n)
                 copy_store(n)

@@ -29,8 +29,8 @@ BMOD = 4
 BPH = 3
 BQ = 64
 BZ = 63
-B_SET = (7, 10, 13, 16, 19, 22, 25, 28, 31, 34, 37, 40, 43, 46, 49, 52, 55, 58, 61)
-PRB = 8
+B_SET = (7, 10, 16, 19, 22, 28, 31, 34, 37, 40, 43, 46, 49, 52, 55, 58, 61)
+PRB = 5
 FIRST_B = (0,)
 GROUP = 3
 DMOD = 64
@@ -38,13 +38,13 @@ DPH = ()
 D_FROM = 10
 D_TO = 58
 LAGD = 2
-E_SET = (12, 30, 48)
+E_SET = (12, 24, 36)
 TAIL = 2
-MERGE = False
+MERGE = True
 M_FROM = 6
-M_TO = 60
-PAIRB = 4
-RESB = 8
+M_TO = 51
+PAIRB = 3
+RESB = 6
 BSTORE = True
 HALVES = ()
 VSTORE = True

@@ -48,13 +48,17 @@ RESB = 6
 BSTORE = True
 HALVES = ()
 VSTORE = True
-LASTB = (61,)
+LASTB = (61, 62)
 UTB = 4
+SLATE = True
+BORD = ()
+AORD = 0
+ZHB = 2
 XSORT = True
 PSM = 3
 LAGB = 1
 START = 'm1 m0 m2 t1 m3 m4 t2 t3 m5'
-SIDE = '15:g0 18:g1 21:g2 24:g3 9:s4 12:s5 12:x4 15:s6 15:x5 18:s7 18:x6 21:x7 24:q 27:b1'
+SIDE = '15:g0 18:g1 21:g2 24:g3 9:s4 12:s5 12:x4 15:s6 15:x5 18:s7 18:x6 21:x7 24<q 27:b1'
 VADD_FROM = 63
 
 
@@ -80,13 +84,25 @@ def plan():
     while u < 64 or prev or any(prevb) or any(prevd):
         new = list(range(u, min(64, u + GROUP)))
         u += len(new)
-        out += ["m%d" % v for v in new]
-        out += ["t%d" % v for v in prev]
+        out += ["m%d" % v for v in (sorted(new, key=lambda v: kind(v) not in BORD) if BORD else new)]
+        for item in pend:
+            if "<" in item:
+                at, tok = item.split("<")
+                if u - len(new) <= int(at) < u:
+                    out.append(tok)
+        if AORD and len(prevb) >= LAGB:
+            out += ["a%d" % v for v in prevb.pop(0)]
+            out += ["t%d" % v for v in prev]
+            prevb.insert(0, [])
+        else:
+            out += ["t%d" % v for v in prev]
         if len(prevb) >= LAGB or not new:
             out += ["a%d" % v for v in prevb.pop(0)]
         if len(prevd) >= LAGD or not new:
             out += ["a%d" % v for v in prevd.pop(0)]
         for item in pend:
+            if "<" in item:
+                continue
             at, tok = item.split(":")
             if u - len(new) <= int(at) < u:
                 out.append(tok)
@@ -132,7 +148,7 @@ def tile_differentialselfattention_pa_kernel(
         prod_pool = ctx.enter_context(tc.tile_pool(name="prod", bufs=PRB))
         pair_pool = ctx.enter_context(tc.tile_pool(name="pair", bufs=PAIRB))
         z_pool = ctx.enter_context(tc.tile_pool(name="zp", bufs=3))
-        zh_pool = ctx.enter_context(tc.tile_pool(name="zh", bufs=4))
+        zh_pool = ctx.enter_context(tc.tile_pool(name="zh", bufs=ZHB))
         oc_pool = ctx.enter_context(tc.tile_pool(name="oc", bufs=2))
         res_pool = ctx.enter_context(tc.tile_pool(name="res", bufs=RESB))
         psum_m = ctx.enter_context(tc.psum_pool(name="psm", bufs=PSM))
@@ -205,9 +221,12 @@ def tile_differentialselfattention_pa_kernel(
         nc.vector.memset(plane[0][:].bitcast(I32), 0)
         load_x(0)
         load_x(1)
-        load_scales(0)
+        if not SLATE:
+            load_scales(0)
         load_x(2)
         load_x(3)
+        if SLATE:
+            load_scales(0)
         load_words(0)
         nc.vector.memset(idle_words[:], 0.0)
         nc.vector.memset(zero1[:], 0.0)

@@ -22,7 +22,7 @@ C1 = int(TWO_PI * 8192.0) / 8192.0
 C2 = TWO_PI - C1
 
 WARM0 = 5
-HEAD = "a0 A0 a1 a2 a3 g0 g1 g2 g3 x0 V0 x1 i1 V1 q0 A1 q1 A2 x2 S2 q2 A3 x3 S3 q3 b i2 B cV sS"
+HEAD = 'a0 A0 a1 a2 a3 g0 g1 g2 g3 x0 V0 x1 V1 x2 q0 S2 xl3 xh3 Sl3 q1 Vh3 q2 ql3 qh3 b i2 B cS sV A1 A2 A3'
 B_FROM = 99
 B_TO = 63
 BMOD = 4
@@ -38,18 +38,22 @@ DPH = ()
 D_FROM = 10
 D_TO = 58
 LAGD = 2
-E_SET = (12, 24, 36)
+E_SET = (12, 24, 36, 48)
 TAIL = 2
 MERGE = True
-M_FROM = 6
-M_TO = 51
+PKINDS = ('A', 'E')
+M_FROM = 2
+M_TO = 57
 PAIRB = 3
 RESB = 6
 BSTORE = True
-HALVES = ()
+HALVES = (3,)
 VSTORE = True
 LASTB = (61, 62)
 UTB = 4
+MULTAIL = 2
+PAIRDMA = True
+DUMMY = 0
 SLATE = True
 BORD = ()
 AORD = 0
@@ -122,7 +126,7 @@ def pairs():
                 todo = []
             if token[0] == "t":
                 n = int(token[1:])
-                if kind(n) == "A" and M_FROM <= n < M_TO:
+                if kind(n) in PKINDS and M_FROM <= n < M_TO:
                     todo.append(n)
                     if len(todo) == 2:
                         out[todo[0]], out[todo[1]] = todo[1], todo[0]
@@ -474,12 +478,15 @@ def tile_differentialselfattention_pa_kernel(
                 xp = live[("xx", first)][:, 0:4] if u == first else live[("xx", first)][:, 4:8]
             else:
                 xp = prod_pool.tile([P, 4, 2, 2, 64], F32, name="xp", tag="xp")[:]
-            nc.vector.tensor_tensor(
-                out=xp.rearrange("p j q w i -> p j q (w i)"),
-                in0=o[:].to_broadcast([P, 4, 2, P]),
-                in1=table[u // 32][:].rearrange("p j q w i -> p j q (w i)"),
-                op=ALU.mult,
-            )
+            n = 4 // (MULTAIL if u == 63 else 1)
+            for a in range(0, 4, n):
+                js = slice(a, a + n)
+                nc.vector.tensor_tensor(
+                    out=xp[:, js].rearrange("p j q w i -> p j q (w i)"),
+                    in0=o[:, js].to_broadcast([P, n, 2, P]),
+                    in1=table[u // 32][:, js].rearrange("p j q w i -> p j q (w i)"),
+                    op=ALU.mult,
+                )
             if u not in PAIRED:
                 live[("x", u)] = xp
 
@@ -487,14 +494,21 @@ def tile_differentialselfattention_pa_kernel(
             o = live.pop(("o", u))
             oc = oc_pool.tile([P, 4, 1, P], F32, name="oc", tag="oc")
             nc.scalar.copy(out=oc[:], in_=o[:])
-            xp = prod_pool.tile([P, 4, 2, 2, 64], F32, name="xp", tag="xp")
+            if u in PAIRED:
+                first = min(u, PAIRED[u])
+                if ("xx", first) not in live:
+                    live[("xx", first)] = pair_pool.tile([P, 8, 2, 2, 64], F32, name="xx", tag="xx")
+                xp = live[("xx", first)][:, 0:4] if u == first else live[("xx", first)][:, 4:8]
+            else:
+                xp = prod_pool.tile([P, 4, 2, 2, 64], F32, name="xp", tag="xp")[:]
             nc.gpsimd.tensor_tensor(
-                out=xp[:].rearrange("p j q w i -> p j q (w i)"),
+                out=xp.rearrange("p j q w i -> p j q (w i)"),
                 in0=oc[:].to_broadcast([P, 4, 2, P]),
                 in1=table[u // 32][:].rearrange("p j q w i -> p j q (w i)"),
                 op=ALU.mult,
             )
-            live[("x", u)] = xp[:]
+            if u not in PAIRED:
+                live[("x", u)] = xp
 
         def store_part(u, r, a, n):
             h, s = u // 32, u % 32
@@ -528,8 +542,17 @@ def tile_differentialselfattention_pa_kernel(
             xx = live.pop(("xx", u))
             r = res_pool.tile([P, 8, 2, 64], F32, name="rr", tag="rr")
             nc.gpsimd.tensor_tensor(out=r[:], in0=xx[:, :, 0, :, :], in1=xx[:, :, 1, ::-1, :], op=ALU.add)
-            store_part(u, r[:, 0:4].rearrange("p j w i -> p j (w i)"), 0, 4)
-            store_part(v, r[:, 4:8].rearrange("p j w i -> p j (w i)"), 0, 4)
+            s = u % 32
+            if PAIRDMA and v == u + 2 and u // 32 == v // 32 and s // 16 == (s + 2) // 16:
+                h, w, sp = u // 32, s // 16, s % 16
+                head, part = sp // 2, sp % 2
+                nc.sync.dma_start(
+                    out=outs[2 * w + part][0, head : head + 2].rearrange("c (p j) d -> p c j d", j=8)[:, :, 4 * h : 4 * h + 4, :],
+                    in_=r[:].rearrange("p (c j) w i -> p c j (w i)", c=2),
+                )
+            else:
+                store_part(u, r[:, 0:4].rearrange("p j w i -> p j (w i)"), 0, 4)
+                store_part(v, r[:, 4:8].rearrange("p j w i -> p j (w i)"), 0, 4)
 
         def zmul(u):
             h, s = u // 32, u % 32
@@ -583,6 +606,9 @@ def tile_differentialselfattention_pa_kernel(
                 z0 = z[:, 0, :]
                 z1 = z[:, 1, :]
             ob = psum_o.tile([P, 4, P], F32, name="ob", tag="o")
+            if DUMMY:
+                flat = ob[:].rearrange("p j t -> p (j t)")
+                nc.tensor.matmul(flat[:, 0:DUMMY], lhsT=idle_in[:, 0:P], rhs=idle_in[:, 0:DUMMY], start=True, stop=True)
             for jj in range(4):
                 cols = slice(P * jj, P * (jj + 1))
                 nc.tensor.matmul(

@@ -49,7 +49,7 @@ RESB = 6
 BSTORE = True
 HALVES = (3,)
 VSTORE = True
-LASTB = (61, 62)
+LASTB = (60, 61, 62)
 UTB = 4
 MULTAIL = 2
 PAIRDMA = True

from contextlib import ExitStack

import concourse.mybir as mybir
from concourse.masks import make_identity

F32 = mybir.dt.float32
BF16 = mybir.dt.bfloat16
I32 = mybir.dt.int32
U32 = mybir.dt.uint32
U8 = mybir.dt.uint8
E5X4 = mybir.dt.float8_e5m2_x4
E2X4 = mybir.dt.float4_e2m1fn_x4
ACT = mybir.ActivationFunctionType
ALU = mybir.AluOpType

FLOPS = 2 * 1024 * 1024 * 4096

P = 128
TWO_PI = 6.283185307179586
HALF_PI = 1.5707963267948966
C1 = int(TWO_PI * 8192.0) / 8192.0
C2 = TWO_PI - C1

WARM0 = 5
HEAD = 'a0 A0 a1 a2 a3 g0 g1 g2 g3 x0 V0 x1 V1 x2 q0 S2 xl3 xh3 Sl3 q1 Vh3 q2 ql3 qh3 b i2 B cS sV A1 A2 A3'
B_FROM = 99
B_TO = 63
BMOD = 4
BPH = 3
BQ = 64
BZ = 63
B_SET = (7, 10, 16, 19, 22, 28, 31, 34, 37, 40, 43, 46, 49, 52, 55, 58, 61)
PRB = 5
FIRST_B = (0,)
GROUP = 3
DMOD = 64
DPH = ()
D_FROM = 10
D_TO = 58
LAGD = 2
E_SET = (12, 24, 36, 48)
TAIL = 2
MERGE = True
PKINDS = ('A', 'E')
M_FROM = 2
M_TO = 57
PAIRB = 3
RESB = 6
BSTORE = True
HALVES = (3,)
VSTORE = True
LASTB = (60, 61, 62)
UTB = 4
MULTAIL = 2
PAIRDMA = True
DUMMY = 0
SLATE = True
BORD = ()
AORD = 0
ZHB = 2
XSORT = True
PSM = 3
LAGB = 1
START = 'm1 m0 m2 t1 m3 m4 t2 t3 m5'
SIDE = '15:g0 18:g1 21:g2 24:g3 9:s4 12:s5 12:x4 15:s6 15:x5 18:s7 18:x6 21:x7 24<q 27:b1'
VADD_FROM = 63


def kind(u):
    if u in B_SET or u in FIRST_B or (u % BMOD == BPH and B_FROM <= u < B_TO and (u // 3) % BQ != BZ) or u in LASTB:
        return "B"
    if u % DMOD in DPH and D_FROM <= u < D_TO:
        return "D"
    if u in E_SET:
        return "E"
    return "A"


def plan():
    out = START.split()
    u = max(int(x[1:]) for x in out if x[0] == "m") + 1
    done = set(x for x in out)
    prev = [v for v in range(u) if ("t%d" % v) not in done and kind(v) in ("A", "E")]
    prevb = [[v for v in range(u) if ("a%d" % v) not in done and kind(v) == "B"]]
    prevd = [[]]
    pend = list(SIDE.split())
    k = 0
    while u < 64 or prev or any(prevb) or any(prevd):
        new = list(range(u, min(64, u + GROUP)))
        u += len(new)
        out += ["m%d" % v for v in (sorted(new, key=lambda v: kind(v) not in BORD) if BORD else new)]
        for item in pend:
            if "<" in item:
                at, tok = item.split("<")
                if u - len(new) <= int(at) < u:
                    out.append(tok)
        if AORD and len(prevb) >= LAGB:
            out += ["a%d" % v for v in prevb.pop(0)]
            out += ["t%d" % v for v in prev]
            prevb.insert(0, [])
        else:
            out += ["t%d" % v for v in prev]
        if len(prevb) >= LAGB or not new:
            out += ["a%d" % v for v in prevb.pop(0)]
        if len(prevd) >= LAGD or not new:
            out += ["a%d" % v for v in prevd.pop(0)]
        for item in pend:
            if "<" in item:
                continue
            at, tok = item.split(":")
            if u - len(new) <= int(at) < u:
                out.append(tok)
        prev = [v for v in new if kind(v) in ("A", "E")]
        prevb.append([v for v in new if kind(v) == "B"])
        prevd.append([v for v in new if kind(v) == "D"])
        k += 1
    return out


def pairs():
    out = {}
    if MERGE:
        todo = []
        for token in plan():
            if token[0] == "m":
                todo = []
            if token[0] == "t":
                n = int(token[1:])
                if kind(n) in PKINDS and M_FROM <= n < M_TO:
                    todo.append(n)
                    if len(todo) == 2:
                        out[todo[0]], out[todo[1]] = todo[1], todo[0]
                        todo = []
    return out


PAIRED = pairs()


def tile_differentialselfattention_pa_kernel(
    tc, x, Wq_words, Wq_scales, bq, Wk_words, Wk_scales, bk, out_0, out_1, out_2, out_3
):
    nc = tc.nc
    outs = (out_0, out_1, out_2, out_3)
    words_in = (Wq_words, Wk_words)
    scales_in = (Wq_scales, Wk_scales)
    bias_in = (bq, bk)

    with ExitStack() as ctx:
        const = ctx.enter_context(tc.tile_pool(name="const", bufs=1))
        ut_pool = ctx.enter_context(tc.tile_pool(name="ut", bufs=UTB))
        prod_pool = ctx.enter_context(tc.tile_pool(name="prod", bufs=PRB))
        pair_pool = ctx.enter_context(tc.tile_pool(name="pair", bufs=PAIRB))
        z_pool = ctx.enter_context(tc.tile_pool(name="zp", bufs=3))
        zh_pool = ctx.enter_context(tc.tile_pool(name="zh", bufs=ZHB))
        oc_pool = ctx.enter_context(tc.tile_pool(name="oc", bufs=2))
        res_pool = ctx.enter_context(tc.tile_pool(name="res", bufs=RESB))
        psum_m = ctx.enter_context(tc.psum_pool(name="psm", bufs=PSM))
        psum_o = ctx.enter_context(tc.psum_pool(name="pso", bufs=8 - PSM))
        ctx.enter_context(tc.manual_schedule())

        x_sb = [const.tile([P, 1024], BF16, name="x%d" % j) for j in range(8)]
        x_half = {}
        for j in HALVES:
            for g in range(2):
                x_half[(j, g)] = const.tile([P, 512], BF16, name="xh%d_%d" % (j, g))
        xg = [const.tile([P, 2, 512], BF16, name="xg%d" % j, align_bytes=64) for j in range(4)]
        xg_late = const.tile([P, 2, 4, 512], BF16, name="xg_late", align_bytes=64)
        xc = [const.tile([P, 2, 512], U32, name="xc%d" % h, align_bytes=64) for h in range(2)]
        xs = [const.tile([P, 2, 512], U8, name="xs%d" % h, align_bytes=64) for h in range(2)]
        runs = ((0, 0, 4), (0, 4, 12), (1, 0, 16))
        w_sb = [const.tile([P, 2, 256 * n], U8, name="w%d_%d" % (w, s0), align_bytes=64) for (w, s0, n) in runs]
        plane = [const.tile([P, 2, P * n], U8, name="pl%d_%d" % (w, s0), align_bytes=64) for (w, s0, n) in runs]
        ident = const.tile([P, P], F32, name="ident")
        perm = const.tile([P, P], F32, name="perm")
        bias_rows = const.tile([P, P], BF16, name="bias_rows")
        bias_rows32 = const.tile([P, P], F32, name="bias_rows32")
        bias_col = const.tile([P, 32], F32, name="bias_col")
        tok_i = const.tile([P, 8, 1], I32, name="tok_i")
        tok = const.tile([P, 8, 1], F32, name="tok")
        freq = const.tile([P, 1, 64], F32, name="freq")
        table = [const.tile([P, 4, 2, 2, 64], F32, name="table%d" % h) for h in range(2)]
        cs_b = [const.tile([P, 2, 512], F32, name="csb%d" % h) for h in range(2)]
        psi = [const.tile([P, 4, 64], F32, name="psi%d" % h) for h in range(2)]
        abs_psi = [const.tile([P, 4, 1, 64], F32, name="absp%d" % h) for h in range(2)]
        zero1 = const.tile([P, 1], F32, name="zero1")
        junk1 = const.tile([P, 1], F32, name="junk1")
        idle_words = const.tile([P, 256], F32, name="idle_words")
        idle_in = idle_words[:].bitcast(BF16)

        x_view = x[0].rearrange("(p j) k -> p j k", j=8)

        def load_x(j):
            if j in HALVES:
                for g in range(2):
                    nc.sync.dma_start(out=x_half[(j, g)][:], in_=x_view[:, j, 512 * g : 512 * (g + 1)])
            else:
                nc.sync.dma_start(out=x_sb[j][:], in_=x_view[:, j, :])

        def load_scales(i):
            w, s0, n = runs[i]
            for q in range(4):
                nc.sync.dma_start(
                    out=plane[i][32 * q : 32 * q + 4, :, :].bitcast(I32),
                    in_=scales_in[w][:, 4 * q : 4 * q + 4, P * s0 : P * (s0 + n)].rearrange("g r n -> r g n").bitcast(I32),
                )

        def load_words(i):
            w, s0, n = runs[i]
            nc.sync.dma_start(
                out=w_sb[i][:].bitcast(I32),
                in_=words_in[w][:, :, 256 * s0 : 256 * (s0 + n)].rearrange("g p n -> p g n").bitcast(I32),
            )

        def run_of(w, sp):
            for i in range(len(runs)):
                if runs[i][0] == w and runs[i][1] <= sp < runs[i][1] + runs[i][2]:
                    return i, sp - runs[i][1]
            return None

        for w in range(2):
            nc.scalar.dma_start(
                out=bias_rows[16 * w : 16 * w + 16, :], in_=bias_in[w].rearrange("(r c) -> r c", c=P)
            )
        nc.vector.memset(plane[0][:].bitcast(I32), 0)
        load_x(0)
        load_x(1)
        if not SLATE:
            load_scales(0)
        load_x(2)
        load_x(3)
        if SLATE:
            load_scales(0)
        load_words(0)
        nc.vector.memset(idle_words[:], 0.0)
        nc.vector.memset(zero1[:], 0.0)
        nc.scalar.activation(out=junk1[:], in_=zero1[:], func=ACT.Sin)
        nc.gpsimd.iota(tok_i[:].rearrange("p j o -> p (j o)"), pattern=[[1, 8]], base=0, channel_multiplier=8)
        make_identity(nc, ident[:])
        nc.gpsimd.memset(plane[1][:].bitcast(F32), 0.0)
        nc.gpsimd.memset(bias_rows[32:64, :], 0.0)
        nc.gpsimd.memset(bias_rows[64:128, :], 0.0)
        for j in range(4, 8):
            load_x(j)
        load_scales(1)
        load_words(1)
        nc.gpsimd.memset(plane[2][:].bitcast(F32), 0.0)
        load_scales(2)
        load_words(2)
        nc.gpsimd.tensor_scalar(
            out=bias_rows32[:], in0=bias_rows[:], scalar1=1.0, scalar2=0.0, op0=ALU.mult, op1=ALU.add
        )
        nc.gpsimd.tensor_copy(out=perm[:, 0:64], in_=ident[:, 64:128])
        nc.gpsimd.tensor_copy(out=perm[:, 64:128], in_=ident[:, 0:64])

        idle_out = {}

        def idle_matmuls(n):
            if n and "t" not in idle_out:
                idle_out["t"] = psum_m.tile([P, 1, 512], F32, name="idle_ps", tag="m")
            for i in range(n):
                nc.tensor.matmul(idle_out["t"][:, 0, :], lhsT=idle_in[:, 0:P], rhs=idle_in, start=True, stop=True)

        idle_matmuls(WARM0)

        nc.vector.memset(freq[:, :, 0:1], 1.0)
        nc.vector.tensor_copy(out=tok[:], in_=tok_i[:])
        for n in (1, 4, 16):
            for q in (1, 2, 3):
                nc.vector.tensor_scalar_mul(
                    out=freq[:, :, q * n : (q + 1) * n], in0=freq[:, :, 0:n], scalar1=10000.0 ** (-q * n / 64.0)
                )

        th = [const.tile([P, 4, 64], F32, name="th%d" % h) for h in range(2)]
        ki = [const.tile([P, 4, 64], I32, name="ki%d" % h) for h in range(2)]
        r1 = [const.tile([P, 4, 64], F32, name="r1%d" % h) for h in range(2)]

        def angle_ops(h):
            js = slice(4 * h, 4 * h + 4)
            return [
                lambda: nc.vector.tensor_tensor(
                    out=th[h][:],
                    in0=tok[:, js, :].to_broadcast([P, 4, 64]),
                    in1=freq[:].to_broadcast([P, 4, 64]),
                    op=ALU.mult,
                ),
                lambda: nc.vector.tensor_scalar(
                    out=ki[h][:], in0=th[h][:], scalar1=1.0 / TWO_PI, scalar2=0.0, op0=ALU.mult, op1=ALU.add
                ),
                lambda: nc.vector.scalar_tensor_tensor(
                    out=r1[h][:], in0=ki[h][:], scalar=-C1, in1=th[h][:], op0=ALU.mult, op1=ALU.add
                ),
                lambda: nc.vector.scalar_tensor_tensor(
                    out=psi[h][:], in0=ki[h][:], scalar=-C2, in1=r1[h][:], op0=ALU.mult, op1=ALU.add
                ),
            ]

        def trig_ops(h):
            t = table[h]
            return [
                lambda: nc.scalar.activation(out=abs_psi[h][:, :, 0, :], in_=psi[h][:], func=ACT.Abs),
                lambda: nc.scalar.activation(out=t[:, :, 1, 0, :], in_=psi[h][:], func=ACT.Sin),
                lambda: nc.scalar.activation(out=t[:, :, 1, 1, :], in_=psi[h][:], func=ACT.Sin, scale=-1.0),
                lambda: nc.scalar.activation(
                    out=t[:, :, 0, :, :],
                    in_=abs_psi[h][:].to_broadcast([P, 4, 2, 64]),
                    func=ACT.Sin,
                    bias=HALF_PI,
                    scale=-1.0,
                ),
            ]

        tb_ps = {}

        def tableb_transpose(h):
            for q in range(2):
                ps = psum_o.tile([P, 4, P], F32, name="tbps", tag="o")
                for jj in range(4):
                    nc.tensor.transpose(
                        ps[:, jj, :], table[h][:, jj, q, :, :].rearrange("p w i -> p (w i)"), ident[:]
                    )
                tb_ps[(h, q)] = ps

        def tableb_copy(h, q, eng):
            src = tb_ps[(h, q)][:].rearrange("p j t -> p (j t)")
            if eng == "V":
                nc.vector.tensor_copy(out=cs_b[h][:, q, :], in_=src)
            else:
                nc.scalar.copy(out=cs_b[h][:, q, :], in_=src)

        xt_tiles = {}
        x_sorted = [const.tile([P, 2, 2, P], F32, name="xsrt%d" % j) for j in range(4)]

        def xprep_sort(j):
            nc.scalar.copy(
                out=x_sorted[j - 4][:], in_=x_sb[j][:].bitcast(F32).rearrange("p (g t u) -> p g u t", g=2, u=2)
            )

        def xprep_transpose(j):
            xt = psum_o.tile([P, 4, P], F32, name="xt", tag="o")
            xw = x_sb[j][:].bitcast(F32)
            for g in range(2):
                for u in range(2):
                    src = x_sorted[j - 4][:, g, u, :] if (XSORT and j >= 4) else xw[:, 256 * g + u : 256 * (g + 1) : 2]
                    nc.tensor.transpose(xt[:, 2 * g + u, :], src, ident[:])
            xt_tiles[j] = xt

        def half_transpose(j, g):
            xt = psum_o.tile([P, 2, P], F32, name="xth", tag="o")
            xw = (x_half[(j, g)][:] if j in HALVES else x_sb[j][:, 512 * g : 512 * (g + 1)]).bitcast(F32)
            for u in range(2):
                nc.tensor.transpose(xt[:, u, :], xw[:, u:256:2], ident[:])
            xt_tiles[(j, g)] = xt

        def half_copy(j, g, eng):
            dst = xg[j][:, g, :].bitcast(F32).rearrange("p (t u) -> p t u", u=2)
            src = xt_tiles[(j, g)][:].rearrange("p u t -> p t u")
            if eng == "V":
                nc.vector.tensor_copy(out=dst, in_=src)
            else:
                nc.scalar.copy(out=dst, in_=src)

        def half_quant(j, g):
            nc.vector.quantize_mx(
                out=xc[0][:, g, P * j : P * (j + 1)].bitcast(E5X4),
                scales=xs[0][:, g, P * j : P * (j + 1)],
                in_=xg[j][:, g, :],
            )

        def xprep_copy(j, eng="S"):
            dst = xg[j][:] if j < 4 else xg_late[:, :, j - 4, :]
            dst = dst.bitcast(F32).rearrange("p g (t u) -> p g t u", u=2)
            src = xt_tiles[j][:].rearrange("p (g u) t -> p g t u", u=2)
            if eng == "V":
                nc.vector.tensor_copy(out=dst, in_=src)
            else:
                nc.scalar.copy(out=dst, in_=src)

        def xquant(j):
            for g in range(2):
                nc.vector.quantize_mx(
                    out=xc[0][:, g, P * j : P * (j + 1)].bitcast(E5X4),
                    scales=xs[0][:, g, P * j : P * (j + 1)],
                    in_=xg[j][:, g, :],
                )

        def xquant_late():
            nc.vector.quantize_mx(
                out=xc[1][:].rearrange("p g c -> p (g c)").bitcast(E5X4),
                scales=xs[1][:].rearrange("p g c -> p (g c)"),
                in_=xg_late[:].rearrange("p g j c -> p (g j c)"),
            )

        a0, a1 = angle_ops(0), angle_ops(1)
        tg0 = trig_ops(0)

        def head(token):
            c, rest = token[0], token[1:]
            if rest[0:1] in ("l", "h"):
                j, g = int(rest[1:]), 0 if rest[0] == "l" else 1
                if c == "x":
                    half_transpose(j, g)
                elif c == "q":
                    half_quant(j, g)
                else:
                    half_copy(j, g, c)
                return
            if c == "a":
                a0[int(rest)]()
            elif c == "A":
                a1[int(rest)]()
            elif c == "g":
                tg0[int(rest)]()
            elif c == "x":
                xprep_transpose(int(rest))
            elif c == "i":
                idle_matmuls(int(rest))
            elif c == "S":
                xprep_copy(int(rest), "S")
            elif c == "V":
                xprep_copy(int(rest), "V")
            elif c == "q":
                xquant(int(rest))
            elif c == "b":
                tableb_transpose(0)
            elif c == "c":
                tableb_copy(0, 0, rest)
            elif c == "s":
                tableb_copy(0, 1, rest)
            elif c == "B":
                ps = psum_o.tile([P, P], F32, name="bias_ps", tag="o")
                nc.tensor.transpose(ps[:], bias_rows32[:], ident[:])
                nc.scalar.copy(out=bias_col[:], in_=ps[:, 0:32])

        for token in HEAD.split():
            head(token)

        live = {}

        def mx(u):
            h, s = u // 32, u % 32
            w, sp = s // 16, s % 16
            i, sl = run_of(w, sp)
            acc = psum_m.tile([P, 1, 512], F32, name="acc", tag="m")
            for g in range(2):
                nc.tensor.matmul_mx(
                    out=acc[:, 0, :],
                    lhsT=w_sb[i][:, g, 256 * sl : 256 * (sl + 1)].bitcast(E2X4),
                    lhsT_scale=plane[i][:, g, P * sl : P * (sl + 1)],
                    rhs=xc[h][:, g, :].bitcast(E5X4),
                    rhs_scale=xs[h][:, g, :],
                    start=(g == 0),
                    stop=(g == 1),
                )
            live[("acc", u)] = acc

        def evac(u):
            s = u % 32
            ut = ut_pool.tile([P, 512], F32, name="ut", tag="ut")
            nc.scalar.activation(
                out=ut[:], in_=live.pop(("acc", u))[:, 0, :], func=ACT.Identity, bias=bias_col[:, s : s + 1], scale=1.0
            )
            live[("ut", u)] = ut

        def tr(u):
            ut = live.pop(("ut", u))
            o = psum_o.tile([P, 4, 1, P], F32, name="o", tag="o")
            for jj in range(4):
                nc.tensor.transpose(o[:, jj, 0, :], ut[:, P * jj : P * (jj + 1)], ident[:])
            live[("o", u)] = o

        def mul(u):
            o = live.pop(("o", u))
            if u in PAIRED:
                first = min(u, PAIRED[u])
                if ("xx", first) not in live:
                    live[("xx", first)] = pair_pool.tile([P, 8, 2, 2, 64], F32, name="xx", tag="xx")
                xp = live[("xx", first)][:, 0:4] if u == first else live[("xx", first)][:, 4:8]
            else:
                xp = prod_pool.tile([P, 4, 2, 2, 64], F32, name="xp", tag="xp")[:]
            n = 4 // (MULTAIL if u == 63 else 1)
            for a in range(0, 4, n):
                js = slice(a, a + n)
                nc.vector.tensor_tensor(
                    out=xp[:, js].rearrange("p j q w i -> p j q (w i)"),
                    in0=o[:, js].to_broadcast([P, n, 2, P]),
                    in1=table[u // 32][:, js].rearrange("p j q w i -> p j q (w i)"),
                    op=ALU.mult,
                )
            if u not in PAIRED:
                live[("x", u)] = xp

        def mul_gpsimd(u):
            o = live.pop(("o", u))
            oc = oc_pool.tile([P, 4, 1, P], F32, name="oc", tag="oc")
            nc.scalar.copy(out=oc[:], in_=o[:])
            if u in PAIRED:
                first = min(u, PAIRED[u])
                if ("xx", first) not in live:
                    live[("xx", first)] = pair_pool.tile([P, 8, 2, 2, 64], F32, name="xx", tag="xx")
                xp = live[("xx", first)][:, 0:4] if u == first else live[("xx", first)][:, 4:8]
            else:
                xp = prod_pool.tile([P, 4, 2, 2, 64], F32, name="xp", tag="xp")[:]
            nc.gpsimd.tensor_tensor(
                out=xp.rearrange("p j q w i -> p j q (w i)"),
                in0=oc[:].to_broadcast([P, 4, 2, P]),
                in1=table[u // 32][:].rearrange("p j q w i -> p j q (w i)"),
                op=ALU.mult,
            )
            if u not in PAIRED:
                live[("x", u)] = xp

        def store_part(u, r, a, n):
            h, s = u // 32, u % 32
            w, sp = s // 16, s % 16
            head, part = sp // 2, sp % 2
            (nc.scalar if VSTORE and u >= VADD_FROM else nc.sync).dma_start(
                out=outs[2 * w + part][0, head].rearrange("(p j) d -> p j d", j=8)[:, 4 * h + a : 4 * h + a + n, :],
                in_=r,
            )

        def store(u, r):
            h, s = u // 32, u % 32
            w, sp = s // 16, s % 16
            head, part = sp // 2, sp % 2
            (nc.scalar if BSTORE else nc.sync).dma_start(
                out=outs[2 * w + part][0, head].rearrange("(p j) d -> p j d", j=8)[:, 4 * h : 4 * h + 4, :],
                in_=r,
            )

        def add_store(u):
            xp = live.pop(("x", u))
            r = res_pool.tile([P, 4, 2, 64], F32, name="r", tag="r")
            eng = nc.vector if u >= VADD_FROM else nc.gpsimd
            n = 4 // (TAIL if u == 63 else 1)
            for a in range(0, 4, n):
                js = slice(a, a + n)
                eng.tensor_tensor(out=r[:, js], in0=xp[:, js, 0, :, :], in1=xp[:, js, 1, ::-1, :], op=ALU.add)
                store_part(u, r[:, js].rearrange("p j w i -> p j (w i)"), a, n)

        def add_store_pair(u, v):
            xx = live.pop(("xx", u))
            r = res_pool.tile([P, 8, 2, 64], F32, name="rr", tag="rr")
            nc.gpsimd.tensor_tensor(out=r[:], in0=xx[:, :, 0, :, :], in1=xx[:, :, 1, ::-1, :], op=ALU.add)
            s = u % 32
            if PAIRDMA and v == u + 2 and u // 32 == v // 32 and s // 16 == (s + 2) // 16:
                h, w, sp = u // 32, s // 16, s % 16
                head, part = sp // 2, sp % 2
                nc.sync.dma_start(
                    out=outs[2 * w + part][0, head : head + 2].rearrange("c (p j) d -> p c j d", j=8)[:, :, 4 * h : 4 * h + 4, :],
                    in_=r[:].rearrange("p (c j) w i -> p c j (w i)", c=2),
                )
            else:
                store_part(u, r[:, 0:4].rearrange("p j w i -> p j (w i)"), 0, 4)
                store_part(v, r[:, 4:8].rearrange("p j w i -> p j (w i)"), 0, 4)

        def zmul(u):
            h, s = u // 32, u % 32
            acc = live.pop(("acc", u))
            z = z_pool.tile([P, 2, 512], F32, name="z", tag="z")
            nc.vector.scalar_tensor_tensor(
                out=z[:],
                in0=acc[:].to_broadcast([P, 2, 512]),
                scalar=bias_col[:, s : s + 1],
                in1=cs_b[h][:],
                op0=ALU.add,
                op1=ALU.mult,
            )
            live[("z", u)] = z

        def zmul_cos(u):
            h, s = u // 32, u % 32
            acc = live.pop(("acc", u))
            zc = zh_pool.tile([P, 512], F32, name="zc", tag="zc")
            nc.vector.scalar_tensor_tensor(
                out=zc[:],
                in0=acc[:, 0, :],
                scalar=bias_col[:, s : s + 1],
                in1=cs_b[h][:, 0, :],
                op0=ALU.add,
                op1=ALU.mult,
            )
            live[("zc", u)] = zc

        def evac_keep(u):
            s = u % 32
            ut = ut_pool.tile([P, 512], F32, name="ut", tag="ut")
            nc.scalar.activation(
                out=ut[:], in_=live[("acc", u)][:, 0, :], func=ACT.Identity, bias=bias_col[:, s : s + 1], scale=1.0
            )
            live[("ut", u)] = ut

        def zmul_sin(u):
            h = u // 32
            ut = live.pop(("ut", u))
            zs = zh_pool.tile([P, 512], F32, name="zs", tag="zs")
            nc.gpsimd.tensor_tensor(out=zs[:], in0=ut[:], in1=cs_b[h][:, 1, :], op=ALU.mult)
            live[("zs", u)] = zs

        def tradd(u):
            if kind(u) == "D":
                z0 = live.pop(("zc", u))[:]
                z1 = live.pop(("zs", u))[:]
            else:
                z = live.pop(("z", u))
                z0 = z[:, 0, :]
                z1 = z[:, 1, :]
            ob = psum_o.tile([P, 4, P], F32, name="ob", tag="o")
            if DUMMY:
                flat = ob[:].rearrange("p j t -> p (j t)")
                nc.tensor.matmul(flat[:, 0:DUMMY], lhsT=idle_in[:, 0:P], rhs=idle_in[:, 0:DUMMY], start=True, stop=True)
            for jj in range(4):
                cols = slice(P * jj, P * (jj + 1))
                nc.tensor.matmul(
                    ob[:, jj, :], lhsT=z0[:, cols], rhs=ident[:], start=True, stop=False, is_transpose=True
                )
                nc.tensor.matmul(
                    ob[:, jj, :], lhsT=z1[:, cols], rhs=perm[:], start=False, stop=True, is_transpose=True
                )
            live[("ob", u)] = ob

        def copy_store(u):
            ob = live.pop(("ob", u))
            r = res_pool.tile([P, 4, P], F32, name="rb", tag="rb")
            nc.scalar.copy(out=r[:], in_=ob[:])
            store(u, r[:])

        trig1 = trig_ops(1)

        def do(token):
            c, n = token[0], int(token[1:] or "0")
            if c == "m":
                mx(n)
                if kind(n) == "B":
                    zmul(n)
                elif kind(n) == "D":
                    evac_keep(n)
                    zmul_cos(n)
                    zmul_sin(n)
                else:
                    evac(n)
            elif c == "t":
                tr(n)
                if kind(n) == "E":
                    mul_gpsimd(n)
                else:
                    mul(n)
                if n not in PAIRED:
                    add_store(n)
                elif PAIRED[n] < n:
                    add_store_pair(PAIRED[n], n)
            elif c == "a":
                tradd(n)
                copy_store(n)
            elif c == "x":
                xprep_transpose(n)
                xprep_copy(n)
            elif c == "s":
                xprep_sort(n)
            elif c == "q":
                xquant_late()
            elif c == "b":
                tableb_transpose(n)
                tableb_copy(n, 0, "S")
                tableb_copy(n, 1, "S")
            elif c == "g":
                trig1[n]()

        for token in plan():
            do(token)
